import numpy as np
import ml_dtypes


def mxq(x, axis, fmt="e4m3"):
    dtype, down = {"e4m3": (ml_dtypes.float8_e4m3fn, 7), "e5m2": (ml_dtypes.float8_e5m2, 14)}[fmt]
    v = np.moveaxis(np.asarray(x, np.float32).astype(ml_dtypes.bfloat16).astype(np.float64), axis, -1)
    blocks = v.reshape(v.shape[:-1] + (-1, 32))
    amax = np.abs(blocks).max(-1, keepdims=True)
    byte = np.maximum(np.where(amax > 0, np.frexp(amax)[1] - 1 + 127, 0) - down, 1)
    scale = np.exp2(byte - 127.0)
    codes = (blocks / scale).astype(np.float32).astype(dtype).astype(np.float64)
    return np.moveaxis((codes * scale).reshape(v.shape), -1, axis)


WIDE = False


def mx_kscale(k):
    if not WIDE:
        return np.ones(k)
    levels = np.array([10, -10, 5, -5, 0])
    a = np.random.permutation(np.resize(levels, k // 512 * 4)).reshape(k // 512, 4)
    idx = np.arange(k)
    return np.exp2(a[idx // 512, idx % 128 // 32])


BF16 = ml_dtypes.bfloat16


def bf(x):
    return np.asarray(x, np.float32).astype(BF16)


def f64(x):
    return np.asarray(x).astype(np.float64)


E2M1 = np.array([0.0, 0.5, 1.0, 1.5, 2.0, 3.0, 4.0, 6.0, -0.0, -0.5, -1.0, -1.5, -2.0, -3.0, -4.0, -6.0])


def pack_weight(w, fmt):
    k, n = w.shape
    w = f64(bf(w)).reshape(k // 32, 32, n)
    amax = np.abs(w).max(1)
    if fmt == "e4m3":
        byte = np.frexp(amax)[1] - 1 + 127 - 7
    else:
        mant, ex = np.frexp(amax / 6.0)
        byte = np.where(mant > 0.5, ex, ex - 1) + 127
    byte = np.clip(np.where(amax > 0, byte, 1), 1, 254)
    scaled = (w * np.exp2(127.0 - byte)[:, None, :]).reshape(k, n).astype(np.float32)
    by_word = np.ascontiguousarray(scaled.reshape(k // 512, 128, 4, n).transpose(0, 1, 3, 2))
    if fmt == "e4m3":
        words = by_word.astype(ml_dtypes.float8_e4m3fn).view(np.uint8)
    else:
        c = by_word.astype(ml_dtypes.float4_e2m1fn).view(np.uint8) & 0xF
        words = c[..., 0::2] | (c[..., 1::2] << 4)
    return np.ascontiguousarray(words), np.ascontiguousarray(byte.astype(np.uint8).reshape(k // 512, 16, n))


def unpack_weight(words, scales, fmt):
    g, p, n, _ = words.shape
    if fmt == "e4m3":
        vals = np.ascontiguousarray(words).view(ml_dtypes.float8_e4m3fn).astype(np.float64)
    else:
        nib = np.empty((g, p, n, 4), np.uint8)
        nib[..., 0::2] = words & 0xF
        nib[..., 1::2] = words >> 4
        vals = E2M1[nib]
    vals = vals * np.repeat(np.exp2(scales.astype(np.float64) - 127.0), 8, axis=1)[..., None]
    return vals.transpose(0, 1, 3, 2).reshape(g * 512, n)


B, N, DIM, H = 1, 128, 2048, 128
HD = DIM // H
R = 1 + 2 * HD
O = H * R
FMT = "e4m3"


def setup_inputs():
    s, t = mx_kscale(DIM), mx_kscale(DIM)
    g = np.ones((H, R))
    g[:, 0] = 2.0
    g[:, 1 + HD:] = t.reshape(H, HD)
    g = g.reshape(O)
    x = bf(np.random.standard_normal((B, DIM, N)) * s[None, :, None])
    Wqkv = np.random.standard_normal((O, DIM)) / np.sqrt(DIM) * g[:, None] / s[None, :]
    Wqkv_words, Wqkv_scales = pack_weight(np.ascontiguousarray(Wqkv.T), FMT)
    bqkv = bf(np.random.standard_normal(O) * 0.1 * g)
    Wp = np.random.standard_normal((DIM, DIM)) * 2.0 / np.sqrt(DIM) / t[None, :]
    Wp_words, Wp_scales = pack_weight(np.ascontiguousarray(Wp.T), FMT)
    bp = bf(np.random.standard_normal(DIM) * 0.1)
    return {"x": x,
            "Wqkv_words": Wqkv_words,
            "Wqkv_scales": Wqkv_scales,
            "bqkv": bqkv,
            "Wp_words": Wp_words,
            "Wp_scales": Wp_scales,
            "bp": bp}


def reference(x, Wqkv_words, Wqkv_scales, bqkv, Wp_words, Wp_scales, bp):
    qkv = (unpack_weight(Wqkv_words, Wqkv_scales, FMT).T @ mxq(f64(x), 1, "e4m3")) + f64(bqkv)[None, :, None]
    qkv = qkv.reshape(B, H, 1 + 2 * HD, N)
    q = qkv[:, :, 0:1, :]
    k = qkv[:, :, 1:1 + HD, :]
    v = qkv[:, :, 1 + HD:, :]
    e = np.exp(q - q.max(-1, keepdims=True))
    scores = e / e.sum(-1, keepdims=True)
    ctx = np.sum(k * scores, axis=-1, keepdims=True)
    out = np.maximum(v, 0.0) * ctx
    out = out.transpose(0, 3, 1, 2).reshape(B, N, H * HD)
    out = out.transpose(0, 2, 1)
    return (unpack_weight(Wp_words, Wp_scales, FMT).T @ mxq(out, 1, "e4m3")) + f64(bp)[None, :, None]

@@ -1,0 +1,241 @@
+from contextlib import ExitStack
+
+import concourse.bass as bass
+import concourse.mybir as mybir
+import concourse.tile as tile
+from concourse.masks import make_identity
+
+F32 = mybir.dt.float32
+BF16 = mybir.dt.bfloat16
+I32 = mybir.dt.int32
+U32 = mybir.dt.uint32
+U8 = mybir.dt.uint8
+FP8X4 = mybir.dt.float8_e4m3fn_x4
+ALU = mybir.AluOpType
+ACT = mybir.ActivationFunctionType
+AX = mybir.AxisListType
+
+P = 128
+N = 128
+DIM = 2048
+H = 128
+HD = 16
+R = 1 + 2 * HD
+O = H * R
+G = DIM // 512
+
+FLOPS = 2 * O * DIM * N + 2 * DIM * DIM * N
+
+
+def plan_tiles():
+    tiles = []
+    h0 = 0
+    for step in range(H):
+        if h0 < H:
+            start = (R * h0) // 64 * 64
+            width = 512
+            if start + width > O:
+                width = 256
+                start = O - width
+            h1 = min(H, (start + width) // R)
+            tiles.append((start, width, h0, h1))
+            h0 = h1
+    return tiles
+
+
+def tile_broadcastattention_w_kernel(tc, x, wq_words, wq_scales, bqkv, wp_words, wp_scales, bp, out):
+    nc = tc.nc
+    tiles = plan_tiles()
+    rounds = [tiles[i : i + 2] for i in range(0, len(tiles), 2)]
+    with ExitStack() as ctx:
+        keep = ctx.enter_context(tc.tile_pool(name="keep", bufs=1))
+        work = ctx.enter_context(tc.tile_pool(name="work", bufs=2))
+        ps_a = ctx.enter_context(tc.psum_pool(name="ps_a", bufs=4))
+        ps_b = ctx.enter_context(tc.psum_pool(name="ps_b", bufs=2))
+        ps_c = ctx.enter_context(tc.psum_pool(name="ps_c", bufs=1))
+        ps_d = ctx.enter_context(tc.psum_pool(name="ps_d", bufs=1))
+
+        wq_pl = keep.tile([P, O], U8, align_bytes=64)
+        wp_pl = keep.tile([P, DIM], U8, align_bytes=64)
+        wq = keep.tile([P, G, O], U32, align_bytes=64)
+        wp = keep.tile([P, G, DIM], U32, align_bytes=64)
+        xraw = keep.tile([P, G, 4 * N], BF16)
+        brow = keep.tile([P, O], BF16)
+        bpt = keep.tile([P, P], BF16)
+
+        nc.vector.memset(wq_pl[:].bitcast(I32), 0)
+        nc.vector.memset(wp_pl[:].bitcast(I32), 0)
+        nc.vector.memset(brow[:], 0.0)
+        nc.gpsimd.memset(bpt[:], 0.0)
+
+        nc.scalar.dma_start(out=xraw[:], in_=x[0].rearrange("(g p j) n -> p g (j n)", g=G, p=P, j=4))
+        nc.scalar.dma_start(out=brow[0:1, :], in_=bqkv.rearrange("(o n) -> o n", o=1))
+        nc.scalar.dma_start(out=bpt[0:16, :], in_=bp.rearrange("(m p) -> m p", p=P))
+
+        for q in range(4):
+            nc.sync.dma_start(
+                out=wq_pl[32 * q : 32 * q + 16, :].bitcast(I32),
+                in_=wq_scales[:, 4 * q : 4 * q + 4, :].bitcast(I32),
+            )
+        wq_src = wq_words.rearrange("g p n t -> p g (n t)")
+        c0 = 0
+        for rnd in rounds:
+            c1 = rnd[-1][0] + rnd[-1][1]
+            nc.sync.dma_start(out=wq[:, :, c0:c1].bitcast(I32), in_=wq_src[:, :, 4 * c0 : 4 * c1].bitcast(I32))
+            c0 = c1
+        for q in range(4):
+            nc.sync.dma_start(
+                out=wp_pl[32 * q : 32 * q + 16, :].bitcast(I32),
+                in_=wp_scales[:, 4 * q : 4 * q + 4, :].bitcast(I32),
+            )
+        wp_src = wp_words.rearrange("g p n t -> p g (n t)")
+        for c in range(2):
+            nc.sync.dma_start(
+                out=wp[:, :, 1024 * c : 1024 * (c + 1)].bitcast(I32),
+                in_=wp_src[:, :, 4096 * c : 4096 * (c + 1)].bitcast(I32),
+            )
+
+        ident_f = keep.tile([P, P], F32)
+        make_identity(nc, ident_f[:])
+        ident_b = keep.tile([P, P], BF16)
+        make_identity(nc, ident_b[:])
+        ones_f = keep.tile([P, P], F32)
+        nc.gpsimd.memset(ones_f[:], 1.0)
+        ones_b = keep.tile([P, P], BF16)
+        nc.gpsimd.memset(ones_b[:], 1.0)
+        q_t = keep.tile([P, len(rounds), P], F32)
+        nc.gpsimd.memset(q_t[:], 0.0)
+        warm_in = keep.tile([P, 1], F32)
+        nc.vector.memset(warm_in[:], 0.0)
+        warm_out = keep.tile([P, 1], F32)
+        nc.scalar.activation(out=warm_out[:], in_=warm_in[:], func=ACT.Exp)
+
+        xg = keep.tile([P, G, N, 4], BF16, align_bytes=64)
+        nc.vector.tensor_copy(out=xg[:], in_=xraw[:].rearrange("p g (j n) -> p g n j", j=4))
+        xw = keep.tile([P, G * N], U32, align_bytes=64)
+        xs = keep.tile([P, G * N], U8, align_bytes=64)
+        nc.vector.quantize_mx(out=xw[:].bitcast(FP8X4), scales=xs[:], in_=xg[:].rearrange("p g n j -> p (g n j)"))
+
+        bias_bc = keep.tile([P, H, 2 * HD], BF16)
+        for start, width, h0, h1 in tiles:
+            off = R * h0 - start
+            pb = ps_a.tile([P, 512], F32, tag="a")
+            nc.tensor.matmul(out=pb[:, 0:width], lhsT=ones_b[:], rhs=brow[:, start : start + width], start=True, stop=True)
+            nc.scalar.copy(
+                out=bias_bc[:, h0:h1, :],
+                in_=pb[:, off : off + R * (h1 - h0)].rearrange("p (h r) -> p h r", r=R)[:, :, 1:R],
+            )
+
+        bps = ps_d.tile([P, 4, P], BF16, tag="d")
+        nc.tensor.transpose(out=bps[:, 0, :], in_=bpt[:], identity=ident_b[:])
+        bp_col = keep.tile([P, 16], F32)
+        nc.vector.tensor_copy(out=bp_col[:], in_=bps[:, 0, 0:16])
+
+        k_sb = keep.tile([P, 4, 4 * H], F32)
+        v_sb = keep.tile([P, 4, 4 * H], F32)
+        h_t = keep.tile([P, 4, 4 * H], BF16)
+        hg = keep.tile([P, G, N, 4], BF16, align_bytes=64)
+        hw = keep.tile([P, G * N], U32, align_bytes=64)
+        hs = keep.tile([P, G * N], U8, align_bytes=64)
+        groups_done = 0
+        for r, rnd in enumerate(rounds):
+            r0 = rnd[0][2]
+            r1 = rnd[-1][3]
+            nr = r1 - r0
+            for start, width, h0, h1 in rnd:
+                off = R * h0 - start
+                pq = ps_a.tile([P, 512], F32, tag="a")
+                for g in range(G):
+                    nc.tensor.matmul_mx(
+                        out=pq[:, 0:width],
+                        lhsT=xw[:, N * g : N * (g + 1)].bitcast(FP8X4),
+                        lhsT_scale=xs[:, N * g : N * (g + 1)],
+                        rhs=wq[:, g, start : start + width].bitcast(FP8X4),
+                        rhs_scale=wq_pl[4 * g : P, start : start + width],
+                        start=(g == 0),
+                        stop=(g == G - 1),
+                    )
+                hv = pq[:, off : off + R * (h1 - h0)].rearrange("p (h r) -> p h r", r=R)
+                nc.scalar.copy(out=q_t[:, r, h0 - r0 : h1 - r0], in_=hv[:, :, 0])
+                nc.vector.tensor_tensor(
+                    out=k_sb[:, :, 4 * h0 : 4 * h1].rearrange("p t (h a) -> p t h a", a=4),
+                    in0=hv[:, :, 1 : 1 + HD].rearrange("p h (a t) -> p t h a", t=4),
+                    in1=bias_bc[:, h0:h1, 0:HD].rearrange("p h (a t) -> p t h a", t=4),
+                    op=ALU.add,
+                )
+                nc.vector.tensor_tensor(
+                    out=v_sb[:, :, 4 * h0 : 4 * h1].rearrange("p t (h a) -> p t h a", a=4),
+                    in0=hv[:, :, 1 + HD : R].rearrange("p h (a t) -> p t h a", t=4),
+                    in1=bias_bc[:, h0:h1, HD : 2 * HD].rearrange("p h (a t) -> p t h a", t=4),
+                    op=ALU.add,
+                )
+            tq = ps_b.tile([P, P], F32, tag="b")
+            nc.tensor.transpose(out=tq[:], in_=q_t[:, r, :], identity=ident_f[:])
+            negmax = work.tile([P, 1], F32)
+            nc.vector.tensor_reduce(out=negmax[:], in_=tq[:], axis=AX.X, op=ALU.max, negate=True)
+            e_sb = work.tile([P, P], F32)
+            esum = work.tile([P, 1], F32)
+            nc.scalar.activation(out=e_sb[:], in_=tq[:], func=ACT.Exp, bias=negmax[:, 0:1], scale=1.0, accum_out=esum[:])
+            rsum = work.tile([P, 1], F32)
+            nc.vector.reciprocal(out=rsum[:], in_=esum[:])
+            s_sb = work.tile([P, P], F32)
+            nc.vector.tensor_scalar_mul(out=s_sb[:], in0=e_sb[:], scalar1=rsum[:, 0:1])
+            s_t = ps_b.tile([P, P], F32, tag="b")
+            nc.tensor.transpose(out=s_t[:], in_=s_sb[:], identity=ident_f[:])
+            prod = work.tile([P, 4, 4 * nr], F32, tag="prod")
+            nc.vector.tensor_tensor(
+                out=prod[:].rearrange("p t (h a) -> p t h a", a=4),
+                in0=k_sb[:, :, 4 * r0 : 4 * r1].rearrange("p t (h a) -> p t h a", a=4),
+                in1=s_t[:, 0:nr].unsqueeze(1).unsqueeze(3).to_broadcast([P, 4, nr, 4]),
+                op=ALU.mult,
+            )
+            cx = ps_c.tile([P, 16 * nr], F32, tag="c")
+            nc.tensor.matmul(out=cx[:], lhsT=ones_f[:], rhs=prod[:].rearrange("p t c -> p (t c)"), start=True, stop=True)
+            nc.vector.scalar_tensor_tensor(
+                out=h_t[:, :, 4 * r0 : 4 * r1],
+                in0=v_sb[:, :, 4 * r0 : 4 * r1],
+                scalar=0.0,
+                in1=cx[:].rearrange("p (t c) -> p t c", t=4),
+                op0=ALU.max,
+                op1=ALU.mult,
+            )
+            for g in range(groups_done, r1 // 32):
+                hp = ps_d.tile([P, 4, P], BF16, tag="d")
+                for t in range(4):
+                    nc.tensor.transpose(out=hp[:, t, :], in_=h_t[:, t, P * g : P * (g + 1)], identity=ident_b[:])
+                nc.scalar.copy(out=hg[:, g, :, :], in_=hp[:].rearrange("p t n -> p n t"))
+                nc.vector.quantize_mx(
+                    out=hw[:, N * g : N * (g + 1)].bitcast(FP8X4),
+                    scales=hs[:, N * g : N * (g + 1)],
+                    in_=hg[:, g, :, :].rearrange("p n t -> p (n t)"),
+                )
+            groups_done = r1 // 32
+
+        out_sb = keep.tile([P, 16, N], F32)
+        out_v = out[0].rearrange("(m p) n -> p m n", p=P)
+        for b in range(4):
+            po = ps_a.tile([P, 4, N], F32, tag="a")
+            for i in range(4):
+                m = 4 * b + i
+                for g in range(G):
+                    nc.tensor.matmul_mx(
+                        out=po[:, i, :],
+                        lhsT=wp[:, g, P * m : P * (m + 1)].bitcast(FP8X4),
+                        lhsT_scale=wp_pl[4 * g : P, P * m : P * (m + 1)],
+                        rhs=hw[:, N * g : N * (g + 1)].bitcast(FP8X4),
+                        rhs_scale=hs[:, N * g : N * (g + 1)],
+                        start=(g == 0),
+                        stop=(g == G - 1),
+                    )
+            if b % 2 == 0:
+                nc.vector.tensor_tensor(
+                    out=out_sb[:, 4 * b : 4 * b + 4, :],
+                    in0=po[:],
+                    in1=bp_col[:, 4 * b : 4 * b + 4].unsqueeze(2).to_broadcast([P, 4, N]),
+                    op=ALU.add,
+                )
+            else:
+                for i in range(4):
+                    m = 4 * b + i
+                    nc.scalar.activation(out=out_sb[:, m, :], in_=po[:, i, :], func=ACT.Identity, bias=bp_col[:, m : m + 1], scale=1.0)
+            nc.sync.dma_start(out=out_v[:, 4 * b : 4 * b + 4, :], in_=out_sb[:, 4 * b : 4 * b + 4, :])

@@ -1,8 +1,6 @@
 from contextlib import ExitStack
 
-import concourse.bass as bass
 import concourse.mybir as mybir
-import concourse.tile as tile
 from concourse.masks import make_identity
 
 F32 = mybir.dt.float32
@@ -23,200 +21,264 @@ HD = 16
 R = 1 + 2 * HD
 O = H * R
 G = DIM // 512
+HR = H // G
+RC = HR * R
+WINDOWS = ((0, 512, 0, 15), (480, 512, 15, 30), (928, 128, 30, 32))
+WP_CHUNKS = ((0, 1024), (1024, 1536), (1536, 2048))
 
 FLOPS = 2 * O * DIM * N + 2 * DIM * DIM * N
 
 
-def plan_tiles():
-    tiles = []
-    h0 = 0
-    for step in range(H):
-        if h0 < H:
-            start = (R * h0) // 64 * 64
-            width = 512
-            if start + width > O:
-                width = 256
-                start = O - width
-            h1 = min(H, (start + width) // R)
-            tiles.append((start, width, h0, h1))
-            h0 = h1
-    return tiles
-
-
 def tile_broadcastattention_w_kernel(tc, x, wq_words, wq_scales, bqkv, wp_words, wp_scales, bp, out):
     nc = tc.nc
-    tiles = plan_tiles()
-    rounds = [tiles[i : i + 2] for i in range(0, len(tiles), 2)]
     with ExitStack() as ctx:
+        ctx.enter_context(tc.manual_schedule())
         keep = ctx.enter_context(tc.tile_pool(name="keep", bufs=1))
         work = ctx.enter_context(tc.tile_pool(name="work", bufs=2))
-        ps_a = ctx.enter_context(tc.psum_pool(name="ps_a", bufs=4))
-        ps_b = ctx.enter_context(tc.psum_pool(name="ps_b", bufs=2))
-        ps_c = ctx.enter_context(tc.psum_pool(name="ps_c", bufs=1))
-        ps_d = ctx.enter_context(tc.psum_pool(name="ps_d", bufs=1))
+        ps_w = ctx.enter_context(tc.psum_pool(name="ps_w", bufs=6))
+        ps_s = ctx.enter_context(tc.psum_pool(name="ps_s", bufs=1))
+        ps_v = ctx.enter_context(tc.psum_pool(name="ps_v", bufs=1))
 
-        wq_pl = keep.tile([P, O], U8, align_bytes=64)
+        pl = keep.tile([P, O], U8, align_bytes=64)
+        pl2 = keep.tile([P, O + 64], U8, align_bytes=64)
         wp_pl = keep.tile([P, DIM], U8, align_bytes=64)
         wq = keep.tile([P, G, O], U32, align_bytes=64)
         wp = keep.tile([P, G, DIM], U32, align_bytes=64)
         xraw = keep.tile([P, G, 4 * N], BF16)
-        brow = keep.tile([P, O], BF16)
+        brow = keep.tile([P, H * HD], BF16)
         bpt = keep.tile([P, P], BF16)
+        bk_col = keep.tile([P, G, 16], BF16)
+        warm_in = keep.tile([P, 1], F32)
+        warm_out = keep.tile([P, 1], F32)
+        ident_f = keep.tile([P, P], F32)
+        ident_b = keep.tile([P, P], BF16)
+        ones_f = keep.tile([P, 2], F32)
+        ones_b = keep.tile([P, P], BF16)
+        q_t = keep.tile([P, G, P], F32)
 
-        nc.vector.memset(wq_pl[:].bitcast(I32), 0)
+        nc.vector.memset(pl[:].bitcast(I32), 0)
         nc.vector.memset(wp_pl[:].bitcast(I32), 0)
-        nc.vector.memset(brow[:], 0.0)
+        nc.vector.memset(warm_in[:], 0.0)
+        nc.gpsimd.memset(brow[:].bitcast(F32), 0.0)
+        nc.gpsimd.dma_start(
+            out=brow[0:1, :].rearrange("o (h d) -> o h d", d=HD),
+            in_=bqkv.rearrange("(o h r) -> o h r", o=1, r=R)[:, :, 1 + HD : R],
+        )
+        nc.gpsimd.memset(ones_b[:], 1.0)
         nc.gpsimd.memset(bpt[:], 0.0)
+        make_identity(nc, ident_b[:])
+        make_identity(nc, ident_f[:])
+        nc.gpsimd.memset(q_t[:], 0.0)
+        nc.gpsimd.memset(ones_f[:], 1.0)
 
         nc.scalar.dma_start(out=xraw[:], in_=x[0].rearrange("(g p j) n -> p g (j n)", g=G, p=P, j=4))
-        nc.scalar.dma_start(out=brow[0:1, :], in_=bqkv.rearrange("(o n) -> o n", o=1))
         nc.scalar.dma_start(out=bpt[0:16, :], in_=bp.rearrange("(m p) -> m p", p=P))
+        nc.scalar.activation(out=warm_out[:], in_=warm_in[:], func=ACT.Exp)
 
         for q in range(4):
             nc.sync.dma_start(
-                out=wq_pl[32 * q : 32 * q + 16, :].bitcast(I32),
+                out=pl[32 * q : 32 * q + 16, :].bitcast(I32),
                 in_=wq_scales[:, 4 * q : 4 * q + 4, :].bitcast(I32),
             )
         wq_src = wq_words.rearrange("g p n t -> p g (n t)")
-        c0 = 0
-        for rnd in rounds:
-            c1 = rnd[-1][0] + rnd[-1][1]
-            nc.sync.dma_start(out=wq[:, :, c0:c1].bitcast(I32), in_=wq_src[:, :, 4 * c0 : 4 * c1].bitcast(I32))
-            c0 = c1
+        for r in range(G):
+            for kg in range(G):
+                nc.sync.dma_start(
+                    out=wq[:, kg, RC * r : RC * (r + 1)].bitcast(I32),
+                    in_=wq_src[:, kg, 4 * RC * r : 4 * RC * (r + 1)].bitcast(I32),
+                )
         for q in range(4):
             nc.sync.dma_start(
                 out=wp_pl[32 * q : 32 * q + 16, :].bitcast(I32),
                 in_=wp_scales[:, 4 * q : 4 * q + 4, :].bitcast(I32),
             )
         wp_src = wp_words.rearrange("g p n t -> p g (n t)")
-        for c in range(2):
-            nc.sync.dma_start(
-                out=wp[:, :, 1024 * c : 1024 * (c + 1)].bitcast(I32),
-                in_=wp_src[:, :, 4096 * c : 4096 * (c + 1)].bitcast(I32),
-            )
-
-        ident_f = keep.tile([P, P], F32)
-        make_identity(nc, ident_f[:])
-        ident_b = keep.tile([P, P], BF16)
-        make_identity(nc, ident_b[:])
-        ones_f = keep.tile([P, P], F32)
-        nc.gpsimd.memset(ones_f[:], 1.0)
-        ones_b = keep.tile([P, P], BF16)
-        nc.gpsimd.memset(ones_b[:], 1.0)
-        q_t = keep.tile([P, len(rounds), P], F32)
-        nc.gpsimd.memset(q_t[:], 0.0)
-        warm_in = keep.tile([P, 1], F32)
-        nc.vector.memset(warm_in[:], 0.0)
-        warm_out = keep.tile([P, 1], F32)
-        nc.scalar.activation(out=warm_out[:], in_=warm_in[:], func=ACT.Exp)
+        for c0, c1 in WP_CHUNKS:
+            nc.sync.dma_start(out=wp[:, :, c0:c1].bitcast(I32), in_=wp_src[:, :, 4 * c0 : 4 * c1].bitcast(I32))
 
         xg = keep.tile([P, G, N, 4], BF16, align_bytes=64)
-        nc.vector.tensor_copy(out=xg[:], in_=xraw[:].rearrange("p g (j n) -> p g n j", j=4))
+        for half in range(2):
+            nc.vector.tensor_copy(
+                out=xg[:, 2 * half : 2 * half + 2, :, :],
+                in_=xraw[:, 2 * half : 2 * half + 2, :].rearrange("p g (j n) -> p g n j", j=4),
+            )
         xw = keep.tile([P, G * N], U32, align_bytes=64)
         xs = keep.tile([P, G * N], U8, align_bytes=64)
-        nc.vector.quantize_mx(out=xw[:].bitcast(FP8X4), scales=xs[:], in_=xg[:].rearrange("p g n j -> p (g n j)"))
-
-        bias_bc = keep.tile([P, H, 2 * HD], BF16)
-        for start, width, h0, h1 in tiles:
-            off = R * h0 - start
-            pb = ps_a.tile([P, 512], F32, tag="a")
-            nc.tensor.matmul(out=pb[:, 0:width], lhsT=ones_b[:], rhs=brow[:, start : start + width], start=True, stop=True)
-            nc.scalar.copy(
-                out=bias_bc[:, h0:h1, :],
-                in_=pb[:, off : off + R * (h1 - h0)].rearrange("p (h r) -> p h r", r=R)[:, :, 1:R],
+        for half in range(2):
+            nc.vector.quantize_mx(
+                out=xw[:, 2 * N * half : 2 * N * (half + 1)].bitcast(FP8X4),
+                scales=xs[:, 2 * N * half : 2 * N * (half + 1)],
+                in_=xg[:, 2 * half : 2 * half + 2, :, :].rearrange("p g n j -> p (g n j)"),
             )
+        nc.vector.tensor_copy(out=pl2[:].bitcast(I32)[:, 8 : 8 + O // 4], in_=pl[:].bitcast(I32))
 
-        bps = ps_d.tile([P, 4, P], BF16, tag="d")
-        nc.tensor.transpose(out=bps[:, 0, :], in_=bpt[:], identity=ident_b[:])
-        bp_col = keep.tile([P, 16], F32)
-        nc.vector.tensor_copy(out=bp_col[:], in_=bps[:, 0, 0:16])
+        bias_v = keep.tile([P, H, HD], BF16)
+        for j in range(4):
+            pb = ps_w.tile([P, 512], F32, tag="w")
+            nc.tensor.matmul(out=pb[:], lhsT=ones_b[:], rhs=brow[:, 512 * j : 512 * (j + 1)], start=True, stop=True)
+            nc.scalar.copy(out=bias_v[:, 32 * j : 32 * (j + 1), :].rearrange("p h d -> p (h d)"), in_=pb[:])
+        bk_src = bqkv.rearrange("(g h r) -> g h r", g=G, r=R)
+        for g in range(G):
+            nc.scalar.dma_start(out=bk_col[:, g, 0:4], in_=bk_src[g, :, 1 : 1 + HD].rearrange("h (a t) -> h a t", t=4))
 
         k_sb = keep.tile([P, 4, 4 * H], F32)
         v_sb = keep.tile([P, 4, 4 * H], F32)
-        h_t = keep.tile([P, 4, 4 * H], BF16)
         hg = keep.tile([P, G, N, 4], BF16, align_bytes=64)
         hw = keep.tile([P, G * N], U32, align_bytes=64)
         hs = keep.tile([P, G * N], U8, align_bytes=64)
-        groups_done = 0
-        for r, rnd in enumerate(rounds):
-            r0 = rnd[0][2]
-            r1 = rnd[-1][3]
-            nr = r1 - r0
-            for start, width, h0, h1 in rnd:
-                off = R * h0 - start
-                pq = ps_a.tile([P, 512], F32, tag="a")
-                for g in range(G):
-                    nc.tensor.matmul_mx(
-                        out=pq[:, 0:width],
-                        lhsT=xw[:, N * g : N * (g + 1)].bitcast(FP8X4),
-                        lhsT_scale=xs[:, N * g : N * (g + 1)],
-                        rhs=wq[:, g, start : start + width].bitcast(FP8X4),
-                        rhs_scale=wq_pl[4 * g : P, start : start + width],
-                        start=(g == 0),
-                        stop=(g == G - 1),
-                    )
-                hv = pq[:, off : off + R * (h1 - h0)].rearrange("p (h r) -> p h r", r=R)
-                nc.scalar.copy(out=q_t[:, r, h0 - r0 : h1 - r0], in_=hv[:, :, 0])
-                nc.vector.tensor_tensor(
-                    out=k_sb[:, :, 4 * h0 : 4 * h1].rearrange("p t (h a) -> p t h a", a=4),
-                    in0=hv[:, :, 1 : 1 + HD].rearrange("p h (a t) -> p t h a", t=4),
-                    in1=bias_bc[:, h0:h1, 0:HD].rearrange("p h (a t) -> p t h a", t=4),
-                    op=ALU.add,
+        win = {}
+
+        def passes(r, kg):
+            for w, (c, width, h0, h1) in enumerate(WINDOWS):
+                if kg == 0:
+                    win[(r, w)] = ps_w.tile([P, 512], F32, tag="w", name="win")
+                col = RC * r + c
+                plane, pc = (pl, col) if col % 64 == 0 else (pl2, col + 32)
+                nc.tensor.matmul_mx(
+                    out=win[(r, w)][:, 0:width],
+                    lhsT=xw[:, N * kg : N * (kg + 1)].bitcast(FP8X4),
+                    lhsT_scale=xs[:, N * kg : N * (kg + 1)],
+                    rhs=wq[:, kg, col : col + width].bitcast(FP8X4),
+                    rhs_scale=plane[4 * kg : P, pc : pc + width],
+                    start=(kg == 0),
+                    stop=(kg == G - 1),
                 )
-                nc.vector.tensor_tensor(
-                    out=v_sb[:, :, 4 * h0 : 4 * h1].rearrange("p t (h a) -> p t h a", a=4),
-                    in0=hv[:, :, 1 + HD : R].rearrange("p h (a t) -> p t h a", t=4),
-                    in1=bias_bc[:, h0:h1, HD : 2 * HD].rearrange("p h (a t) -> p t h a", t=4),
-                    op=ALU.add,
-                )
-            tq = ps_b.tile([P, P], F32, tag="b")
-            nc.tensor.transpose(out=tq[:], in_=q_t[:, r, :], identity=ident_f[:])
-            negmax = work.tile([P, 1], F32)
-            nc.vector.tensor_reduce(out=negmax[:], in_=tq[:], axis=AX.X, op=ALU.max, negate=True)
-            e_sb = work.tile([P, P], F32)
-            esum = work.tile([P, 1], F32)
-            nc.scalar.activation(out=e_sb[:], in_=tq[:], func=ACT.Exp, bias=negmax[:, 0:1], scale=1.0, accum_out=esum[:])
-            rsum = work.tile([P, 1], F32)
-            nc.vector.reciprocal(out=rsum[:], in_=esum[:])
-            s_sb = work.tile([P, P], F32)
-            nc.vector.tensor_scalar_mul(out=s_sb[:], in0=e_sb[:], scalar1=rsum[:, 0:1])
-            s_t = ps_b.tile([P, P], F32, tag="b")
-            nc.tensor.transpose(out=s_t[:], in_=s_sb[:], identity=ident_f[:])
-            prod = work.tile([P, 4, 4 * nr], F32, tag="prod")
+
+        def heads(r, w):
+            c, width, h0, h1 = WINDOWS[w]
+            off = R * h0 - c
+            return win[(r, w)][:, off : off + R * (h1 - h0)].rearrange("p (h r) -> p h r", r=R)
+
+        def q_copy(r, w):
+            c, width, h0, h1 = WINDOWS[w]
+            nc.scalar.copy(out=q_t[:, r, h0:h1], in_=heads(r, w)[:, :, 0])
+
+        def k_copy(r, w):
+            c, width, h0, h1 = WINDOWS[w]
+            nc.scalar.copy(
+                out=k_sb[:, :, 4 * (HR * r + h0) : 4 * (HR * r + h1)].rearrange("p t (h a) -> p t h a", a=4),
+                in_=heads(r, w)[:, :, 1 : 1 + HD].rearrange("p h (a t) -> p t h a", t=4),
+            )
+
+        def v_evac(r, w):
+            c, width, h0, h1 = WINDOWS[w]
             nc.vector.tensor_tensor(
-                out=prod[:].rearrange("p t (h a) -> p t h a", a=4),
-                in0=k_sb[:, :, 4 * r0 : 4 * r1].rearrange("p t (h a) -> p t h a", a=4),
-                in1=s_t[:, 0:nr].unsqueeze(1).unsqueeze(3).to_broadcast([P, 4, nr, 4]),
+                out=v_sb[:, :, 4 * (HR * r + h0) : 4 * (HR * r + h1)].rearrange("p t (h a) -> p t h a", a=4),
+                in0=heads(r, w)[:, :, 1 + HD : R].rearrange("p h (a t) -> p t h a", t=4),
+                in1=bias_v[:, HR * r + h0 : HR * r + h1, :].rearrange("p h (a t) -> p t h a", t=4),
+                op=ALU.add,
+            )
+
+        tl = {}
+
+        def transpose_q(r):
+            tl[("tq", r)] = ps_s.tile([P, P], F32, tag="s", name="tq")
+            nc.tensor.transpose(out=tl[("tq", r)][:], in_=q_t[:, r, :], identity=ident_f[:])
+
+        def row_max(r):
+            tl[("negmax", r)] = work.tile([P, 1], F32, tag="negmax", name="negmax")
+            nc.vector.tensor_reduce(out=tl[("negmax", r)][:], in_=tl[("tq", r)][:], axis=AX.X, op=ALU.max, negate=True)
+
+        def exponent(r):
+            tl[("e", r)] = work.tile([P, P], F32, tag="e", name="e_sb")
+            tl[("esum", r)] = work.tile([P, 1], F32, tag="esum", name="esum")
+            nc.scalar.activation(
+                out=tl[("e", r)][:], in_=tl[("tq", r)][:], func=ACT.Exp, bias=tl[("negmax", r)][:, 0:1], scale=1.0, accum_out=tl[("esum", r)][:]
+            )
+
+        def normalise(r):
+            rsum = work.tile([P, 1], F32, tag="rsum")
+            nc.vector.reciprocal(out=rsum[:], in_=tl[("esum", r)][:])
+            tl[("s", r)] = work.tile([P, P], F32, tag="s_sb", name="s_sb")
+            nc.vector.tensor_scalar_mul(out=tl[("s", r)][:], in0=tl[("e", r)][:], scalar1=rsum[:, 0:1])
+
+        def transpose_s_v(r):
+            tl[("st", r)] = ps_s.tile([P, P], F32, tag="s", name="s_t")
+            nc.tensor.transpose(out=tl[("st", r)][:], in_=tl[("s", r)][:], identity=ident_f[:])
+            tl[("vps", r)] = ps_v.tile([P, 4, P], F32, tag="v", name="vps")
+            for t in range(4):
+                nc.tensor.transpose(out=tl[("vps", r)][:, t, :], in_=v_sb[:, t, P * r : P * (r + 1)], identity=ident_f[:])
+
+        def product(r):
+            tl[("prod", r)] = work.tile([P, 4, P], F32, tag="prod", name="prod")
+            nc.vector.tensor_tensor(
+                out=tl[("prod", r)][:].rearrange("p t (h a) -> p t h a", a=4),
+                in0=k_sb[:, :, P * r : P * (r + 1)].rearrange("p t (h a) -> p t h a", a=4),
+                in1=tl[("st", r)][:, 0:HR].unsqueeze(1).unsqueeze(3).to_broadcast([P, 4, HR, 4]),
                 op=ALU.mult,
             )
-            cx = ps_c.tile([P, 16 * nr], F32, tag="c")
-            nc.tensor.matmul(out=cx[:], lhsT=ones_f[:], rhs=prod[:].rearrange("p t c -> p (t c)"), start=True, stop=True)
+
+        def context(r):
+            tl[("cx", r)] = ps_s.tile([P, 4, 2], F32, tag="s", name="cx")
+            for t in range(4):
+                nc.tensor.matmul(out=tl[("cx", r)][:, t, :], lhsT=tl[("prod", r)][:, t, :], rhs=ones_f[:], start=True, stop=True)
+
+        def context_bias(r):
+            tl[("ctx", r)] = work.tile([P, 4], F32, tag="ctx", name="ctx_sb")
+            nc.vector.tensor_tensor(out=tl[("ctx", r)][:], in0=tl[("cx", r)][:, :, 0], in1=bk_col[:, r, 0:4], op=ALU.add)
+
+        def hidden(r):
             nc.vector.scalar_tensor_tensor(
-                out=h_t[:, :, 4 * r0 : 4 * r1],
-                in0=v_sb[:, :, 4 * r0 : 4 * r1],
+                out=hg[:, r, :, :],
+                in0=tl[("vps", r)][:].rearrange("p t n -> p n t"),
                 scalar=0.0,
-                in1=cx[:].rearrange("p (t c) -> p t c", t=4),
+                in1=tl[("ctx", r)][:].unsqueeze(1).to_broadcast([P, N, 4]),
                 op0=ALU.max,
                 op1=ALU.mult,
             )
-            for g in range(groups_done, r1 // 32):
-                hp = ps_d.tile([P, 4, P], BF16, tag="d")
-                for t in range(4):
-                    nc.tensor.transpose(out=hp[:, t, :], in_=h_t[:, t, P * g : P * (g + 1)], identity=ident_b[:])
-                nc.scalar.copy(out=hg[:, g, :, :], in_=hp[:].rearrange("p t n -> p n t"))
-                nc.vector.quantize_mx(
-                    out=hw[:, N * g : N * (g + 1)].bitcast(FP8X4),
-                    scales=hs[:, N * g : N * (g + 1)],
-                    in_=hg[:, g, :, :].rearrange("p n t -> p (n t)"),
-                )
-            groups_done = r1 // 32
+
+        def quantise_h(r):
+            nc.vector.quantize_mx(
+                out=hw[:, N * r : N * (r + 1)].bitcast(FP8X4),
+                scales=hs[:, N * r : N * (r + 1)],
+                in_=hg[:, r, :, :].rearrange("p n t -> p (n t)"),
+            )
+
+        def next_passes(r, kg):
+            if r + 1 < G:
+                passes(r + 1, kg)
+
+        for kg in range(G):
+            passes(0, kg)
+        bps = ps_v.tile([P, 4, P], BF16, tag="v")
+        nc.tensor.transpose(out=bps[:, 0, :], in_=bpt[:], identity=ident_b[:])
+        bp_col = keep.tile([P, 16], F32)
+        nc.vector.tensor_copy(out=bp_col[:], in_=bps[:, 0, 0:16])
+        for r in range(G):
+            for w in range(3):
+                q_copy(r, w)
+            for w in range(3):
+                v_evac(r, w)
+            for w in range(3):
+                k_copy(r, w)
+            if r > 0:
+                context(r - 1)
+                context_bias(r - 1)
+            next_passes(r, 0)
+            transpose_q(r)
+            row_max(r)
+            exponent(r)
+            if r > 0:
+                hidden(r - 1)
+            next_passes(r, 1)
+            normalise(r)
+            if r > 0:
+                quantise_h(r - 1)
+            next_passes(r, 2)
+            transpose_s_v(r)
+            product(r)
+            next_passes(r, 3)
+        context(G - 1)
+        context_bias(G - 1)
+        hidden(G - 1)
+        quantise_h(G - 1)
 
         out_sb = keep.tile([P, 16, N], F32)
         out_v = out[0].rearrange("(m p) n -> p m n", p=P)
-        for b in range(4):
-            po = ps_a.tile([P, 4, N], F32, tag="a")
-            for i in range(4):
-                m = 4 * b + i
+        for j in range(8):
+            po = ps_w.tile([P, 2, N], F32, tag="w")
+            for i in range(2):
+                m = 2 * j + i
                 for g in range(G):
                     nc.tensor.matmul_mx(
                         out=po[:, i, :],
@@ -227,15 +289,15 @@ def tile_broadcastattention_w_kernel(tc, x, wq_words, wq_scales, bqkv, wp_words,
                         start=(g == 0),
                         stop=(g == G - 1),
                     )
-            if b % 2 == 0:
+            if j % 2 == 0:
                 nc.vector.tensor_tensor(
-                    out=out_sb[:, 4 * b : 4 * b + 4, :],
+                    out=out_sb[:, 2 * j : 2 * j + 2, :],
                     in0=po[:],
-                    in1=bp_col[:, 4 * b : 4 * b + 4].unsqueeze(2).to_broadcast([P, 4, N]),
+                    in1=bp_col[:, 2 * j : 2 * j + 2].unsqueeze(2).to_broadcast([P, 2, N]),
                     op=ALU.add,
                 )
             else:
-                for i in range(4):
-                    m = 4 * b + i
+                for i in range(2):
+                    m = 2 * j + i
                     nc.scalar.activation(out=out_sb[:, m, :], in_=po[:, i, :], func=ACT.Identity, bias=bp_col[:, m : m + 1], scale=1.0)
-            nc.sync.dma_start(out=out_v[:, 4 * b : 4 * b + 4, :], in_=out_sb[:, 4 * b : 4 * b + 4, :])
+            nc.sync.dma_start(out=out_v[:, 2 * j : 2 * j + 2, :], in_=out_sb[:, 2 * j : 2 * j + 2, :])

@@ -80,6 +80,11 @@ def tile_broadcastattention_w_kernel(tc, x, wq_words, wq_scales, bqkv, wp_words,
                 out=pl[32 * q : 32 * q + 16, :].bitcast(I32),
                 in_=wq_scales[:, 4 * q : 4 * q + 4, :].bitcast(I32),
             )
+        for q in range(4):
+            nc.sync.dma_start(
+                out=wp_pl[32 * q : 32 * q + 16, :].bitcast(I32),
+                in_=wp_scales[:, 4 * q : 4 * q + 4, :].bitcast(I32),
+            )
         wq_src = wq_words.rearrange("g p n t -> p g (n t)")
         for r in range(G):
             for kg in range(G):
@@ -87,11 +92,6 @@ def tile_broadcastattention_w_kernel(tc, x, wq_words, wq_scales, bqkv, wp_words,
                     out=wq[:, kg, RC * r : RC * (r + 1)].bitcast(I32),
                     in_=wq_src[:, kg, 4 * RC * r : 4 * RC * (r + 1)].bitcast(I32),
                 )
-        for q in range(4):
-            nc.sync.dma_start(
-                out=wp_pl[32 * q : 32 * q + 16, :].bitcast(I32),
-                in_=wp_scales[:, 4 * q : 4 * q + 4, :].bitcast(I32),
-            )
         wp_src = wp_words.rearrange("g p n t -> p g (n t)")
         for c0, c1 in WP_CHUNKS:
             nc.sync.dma_start(out=wp[:, :, c0:c1].bitcast(I32), in_=wp_src[:, :, 4 * c0 : 4 * c1].bitcast(I32))

@@ -25,6 +25,7 @@ HR = H // G
 RC = HR * R
 WINDOWS = ((0, 512, 0, 15), (480, 512, 15, 30), (928, 128, 30, 32))
 WP_CHUNKS = ((0, 1024), (1024, 1536), (1536, 2048))
+SPLIT_PAIRS = 6
 
 FLOPS = 2 * O * DIM * N + 2 * DIM * DIM * N
 
@@ -35,8 +36,9 @@ def tile_broadcastattention_w_kernel(tc, x, wq_words, wq_scales, bqkv, wp_words,
         ctx.enter_context(tc.manual_schedule())
         keep = ctx.enter_context(tc.tile_pool(name="keep", bufs=1))
         work = ctx.enter_context(tc.tile_pool(name="work", bufs=2))
-        ps_w = ctx.enter_context(tc.psum_pool(name="ps_w", bufs=6))
-        ps_s = ctx.enter_context(tc.psum_pool(name="ps_s", bufs=1))
+        ps_w = ctx.enter_context(tc.psum_pool(name="ps_w", bufs=4))
+        ps_c = ctx.enter_context(tc.psum_pool(name="ps_c", bufs=1))
+        ps_s = ctx.enter_context(tc.psum_pool(name="ps_s", bufs=2))
         ps_v = ctx.enter_context(tc.psum_pool(name="ps_v", bufs=1))
 
         pl = keep.tile([P, O], U8, align_bytes=64)
@@ -128,21 +130,32 @@ def tile_broadcastattention_w_kernel(tc, x, wq_words, wq_scales, bqkv, wp_words,
         hs = keep.tile([P, G * N], U8, align_bytes=64)
         win = {}
 
+        def one_pass(r, w, kg):
+            c, width, h0, h1 = WINDOWS[w]
+            if kg == 0:
+                pool, tag = (ps_w, "w") if w < 2 else (ps_c, "c")
+                win[(r, w)] = pool.tile([P, 512], F32, tag=tag, name="win")
+            col = RC * r + c
+            plane, pc = (pl, col) if col % 64 == 0 else (pl2, col + 32)
+            nc.tensor.matmul_mx(
+                out=win[(r, w)][:, 0:width],
+                lhsT=xw[:, N * kg : N * (kg + 1)].bitcast(FP8X4),
+                lhsT_scale=xs[:, N * kg : N * (kg + 1)],
+                rhs=wq[:, kg, col : col + width].bitcast(FP8X4),
+                rhs_scale=plane[4 * kg : P, pc : pc + width],
+                start=(kg == 0),
+                stop=(kg == G - 1),
+            )
+
         def passes(r, kg):
-            for w, (c, width, h0, h1) in enumerate(WINDOWS):
-                if kg == 0:
-                    win[(r, w)] = ps_w.tile([P, 512], F32, tag="w", name="win")
-                col = RC * r + c
-                plane, pc = (pl, col) if col % 64 == 0 else (pl2, col + 32)
-                nc.tensor.matmul_mx(
-                    out=win[(r, w)][:, 0:width],
-                    lhsT=xw[:, N * kg : N * (kg + 1)].bitcast(FP8X4),
-                    lhsT_scale=xs[:, N * kg : N * (kg + 1)],
-                    rhs=wq[:, kg, col : col + width].bitcast(FP8X4),
-                    rhs_scale=plane[4 * kg : P, pc : pc + width],
-                    start=(kg == 0),
-                    stop=(kg == G - 1),
-                )
+            if r < G:
+                if kg == G - 1:
+                    for early in range(G - 1):
+                        one_pass(r, 2, early)
+                one_pass(r, 0, kg)
+                one_pass(r, 1, kg)
+                if kg == G - 1:
+                    one_pass(r, 2, kg)
 
         def heads(r, w):
             c, width, h0, h1 = WINDOWS[w]
@@ -172,18 +185,21 @@ def tile_broadcastattention_w_kernel(tc, x, wq_words, wq_scales, bqkv, wp_words,
         tl = {}
 
         def transpose_q(r):
-            tl[("tq", r)] = ps_s.tile([P, P], F32, tag="s", name="tq")
-            nc.tensor.transpose(out=tl[("tq", r)][:], in_=q_t[:, r, :], identity=ident_f[:])
+            small = ps_s.tile([P, 512], F32, tag="s")
+            tl[("tq", r)] = small[:, 0:P]
+            tl[("st", r)] = small[:, P : 2 * P]
+            tl[("cx", r)] = small[:, 2 * P : 2 * P + 8].rearrange("p (t two) -> p t two", two=2)
+            nc.tensor.transpose(out=tl[("tq", r)], in_=q_t[:, r, :], identity=ident_f[:])
 
         def row_max(r):
             tl[("negmax", r)] = work.tile([P, 1], F32, tag="negmax", name="negmax")
-            nc.vector.tensor_reduce(out=tl[("negmax", r)][:], in_=tl[("tq", r)][:], axis=AX.X, op=ALU.max, negate=True)
+            nc.vector.tensor_reduce(out=tl[("negmax", r)][:], in_=tl[("tq", r)], axis=AX.X, op=ALU.max, negate=True)
 
         def exponent(r):
             tl[("e", r)] = work.tile([P, P], F32, tag="e", name="e_sb")
             tl[("esum", r)] = work.tile([P, 1], F32, tag="esum", name="esum")
             nc.scalar.activation(
-                out=tl[("e", r)][:], in_=tl[("tq", r)][:], func=ACT.Exp, bias=tl[("negmax", r)][:, 0:1], scale=1.0, accum_out=tl[("esum", r)][:]
+                out=tl[("e", r)][:], in_=tl[("tq", r)], func=ACT.Exp, bias=tl[("negmax", r)][:, 0:1], scale=1.0, accum_out=tl[("esum", r)][:]
             )
 
         def normalise(r):
@@ -192,10 +208,12 @@ def tile_broadcastattention_w_kernel(tc, x, wq_words, wq_scales, bqkv, wp_words,
             tl[("s", r)] = work.tile([P, P], F32, tag="s_sb", name="s_sb")
             nc.vector.tensor_scalar_mul(out=tl[("s", r)][:], in0=tl[("e", r)][:], scalar1=rsum[:, 0:1])
 
-        def transpose_s_v(r):
-            tl[("st", r)] = ps_s.tile([P, P], F32, tag="s", name="s_t")
-            nc.tensor.transpose(out=tl[("st", r)][:], in_=tl[("s", r)][:], identity=ident_f[:])
-            tl[("vps", r)] = ps_v.tile([P, 4, P], F32, tag="v", name="vps")
+        def transpose_s(r):
+            nc.tensor.transpose(out=tl[("st", r)], in_=tl[("s", r)][:], identity=ident_f[:])
+
+        def transpose_v(r):
+            pool, tag = (ps_v, "v") if r < G - 1 else (ps_c, "c")
+            tl[("vps", r)] = pool.tile([P, 4, P], F32, tag=tag, name="vps")
             for t in range(4):
                 nc.tensor.transpose(out=tl[("vps", r)][:, t, :], in_=v_sb[:, t, P * r : P * (r + 1)], identity=ident_f[:])
 
@@ -209,7 +227,6 @@ def tile_broadcastattention_w_kernel(tc, x, wq_words, wq_scales, bqkv, wp_words,
             )
 
         def context(r):
-            tl[("cx", r)] = ps_s.tile([P, 4, 2], F32, tag="s", name="cx")
             for t in range(4):
                 nc.tensor.matmul(out=tl[("cx", r)][:, t, :], lhsT=tl[("prod", r)][:, t, :], rhs=ones_f[:], start=True, stop=True)
 
@@ -234,10 +251,6 @@ def tile_broadcastattention_w_kernel(tc, x, wq_words, wq_scales, bqkv, wp_words,
                 in_=hg[:, r, :, :].rearrange("p n t -> p (n t)"),
             )
 
-        def next_passes(r, kg):
-            if r + 1 < G:
-                passes(r + 1, kg)
-
         for kg in range(G):
             passes(0, kg)
         bps = ps_v.tile([P, 4, P], BF16, tag="v")
@@ -245,57 +258,69 @@ def tile_broadcastattention_w_kernel(tc, x, wq_words, wq_scales, bqkv, wp_words,
         bp_col = keep.tile([P, 16], F32)
         nc.vector.tensor_copy(out=bp_col[:], in_=bps[:, 0, 0:16])
         for r in range(G):
+            last = r == G - 1
             for w in range(3):
                 q_copy(r, w)
             for w in range(3):
                 v_evac(r, w)
             for w in range(3):
                 k_copy(r, w)
-            if r > 0:
-                context(r - 1)
-                context_bias(r - 1)
-            next_passes(r, 0)
+            passes(r + 1, 0)
             transpose_q(r)
             row_max(r)
             exponent(r)
             if r > 0:
-                hidden(r - 1)
-            next_passes(r, 1)
+                transpose_s(r - 1)
+                transpose_v(r - 1)
+                product(r - 1)
+            if last:
+                transpose_v(r)
+            passes(r + 1, 1)
             normalise(r)
+            passes(r + 1, 2)
             if r > 0:
+                context(r - 1)
+                context_bias(r - 1)
+                if last:
+                    transpose_s(r)
+                    product(r)
+                hidden(r - 1)
                 quantise_h(r - 1)
-            next_passes(r, 2)
-            transpose_s_v(r)
-            product(r)
-            next_passes(r, 3)
+            passes(r + 1, 3)
         context(G - 1)
         context_bias(G - 1)
         hidden(G - 1)
         quantise_h(G - 1)
 
         out_sb = keep.tile([P, 16, N], F32)
+        part_sb = keep.tile([P, 2 * SPLIT_PAIRS, N], F32)
         out_v = out[0].rearrange("(m p) n -> p m n", p=P)
+
+        def stage2(dst, m, groups):
+            for g in groups:
+                nc.tensor.matmul_mx(
+                    out=dst,
+                    lhsT=wp[:, g, P * m : P * (m + 1)].bitcast(FP8X4),
+                    lhsT_scale=wp_pl[4 * g : P, P * m : P * (m + 1)],
+                    rhs=hw[:, N * g : N * (g + 1)].bitcast(FP8X4),
+                    rhs_scale=hs[:, N * g : N * (g + 1)],
+                    start=(g == groups[0]),
+                    stop=(g == groups[-1]),
+                )
+
+        for j in range(SPLIT_PAIRS):
+            pa = ps_w.tile([P, 2, N], F32, tag="w")
+            for i in range(2):
+                stage2(pa[:, i, :], 2 * j + i, (0, 1, 2))
+            for i in range(2):
+                m = 2 * j + i
+                nc.scalar.activation(out=part_sb[:, m, :], in_=pa[:, i, :], func=ACT.Identity, bias=bp_col[:, m : m + 1], scale=1.0)
         for j in range(8):
             po = ps_w.tile([P, 2, N], F32, tag="w")
             for i in range(2):
-                m = 2 * j + i
-                for g in range(G):
-                    nc.tensor.matmul_mx(
-                        out=po[:, i, :],
-                        lhsT=wp[:, g, P * m : P * (m + 1)].bitcast(FP8X4),
-                        lhsT_scale=wp_pl[4 * g : P, P * m : P * (m + 1)],
-                        rhs=hw[:, N * g : N * (g + 1)].bitcast(FP8X4),
-                        rhs_scale=hs[:, N * g : N * (g + 1)],
-                        start=(g == 0),
-                        stop=(g == G - 1),
-                    )
-            if j % 2 == 0:
-                nc.vector.tensor_tensor(
-                    out=out_sb[:, 2 * j : 2 * j + 2, :],
-                    in0=po[:],
-                    in1=bp_col[:, 2 * j : 2 * j + 2].unsqueeze(2).to_broadcast([P, 2, N]),
-                    op=ALU.add,
-                )
+                stage2(po[:, i, :], 2 * j + i, (3,) if j < SPLIT_PAIRS else (0, 1, 2, 3))
+            if j < SPLIT_PAIRS:
+                nc.vector.tensor_tensor(out=out_sb[:, 2 * j : 2 * j + 2, :], in0=po[:], in1=part_sb[:, 2 * j : 2 * j + 2, :], op=ALU.add)
             else:
                 for i in range(2):
                     m = 2 * j + i

@@ -24,8 +24,8 @@ G = DIM // 512
 HR = H // G
 RC = HR * R
 WINDOWS = ((0, 512, 0, 15), (480, 512, 15, 30), (928, 128, 30, 32))
-WP_CHUNKS = ((0, 1024), (1024, 1536), (1536, 2048))
-SPLIT_PAIRS = 6
+WP_CHUNKS = ((0, 1024, 0, 4), (1024, 1536, 0, 4), (1536, 2048, 0, 3), (1536, 2048, 3, 4))
+SPLIT_PAIRS = 8
 
 FLOPS = 2 * O * DIM * N + 2 * DIM * DIM * N
 
@@ -67,14 +67,13 @@ def tile_broadcastattention_w_kernel(tc, x, wq_words, wq_scales, bqkv, wp_words,
             in_=bqkv.rearrange("(o h r) -> o h r", o=1, r=R)[:, :, 1 + HD : R],
         )
         nc.gpsimd.memset(ones_b[:], 1.0)
+        nc.gpsimd.memset(q_t[:], 0.0)
+        make_identity(nc, ident_f[:])
+        nc.gpsimd.memset(ones_f[:], 1.0)
         nc.gpsimd.memset(bpt[:], 0.0)
         make_identity(nc, ident_b[:])
-        make_identity(nc, ident_f[:])
-        nc.gpsimd.memset(q_t[:], 0.0)
-        nc.gpsimd.memset(ones_f[:], 1.0)
 
         nc.scalar.dma_start(out=xraw[:], in_=x[0].rearrange("(g p j) n -> p g (j n)", g=G, p=P, j=4))
-        nc.scalar.dma_start(out=bpt[0:16, :], in_=bp.rearrange("(m p) -> m p", p=P))
         nc.scalar.activation(out=warm_out[:], in_=warm_in[:], func=ACT.Exp)
 
         for q in range(4):
@@ -95,8 +94,8 @@ def tile_broadcastattention_w_kernel(tc, x, wq_words, wq_scales, bqkv, wp_words,
                     in_=wq_src[:, kg, 4 * RC * r : 4 * RC * (r + 1)].bitcast(I32),
                 )
         wp_src = wp_words.rearrange("g p n t -> p g (n t)")
-        for c0, c1 in WP_CHUNKS:
-            nc.sync.dma_start(out=wp[:, :, c0:c1].bitcast(I32), in_=wp_src[:, :, 4 * c0 : 4 * c1].bitcast(I32))
+        for c0, c1, g0, g1 in WP_CHUNKS:
+            nc.sync.dma_start(out=wp[:, g0:g1, c0:c1].bitcast(I32), in_=wp_src[:, g0:g1, 4 * c0 : 4 * c1].bitcast(I32))
 
         xg = keep.tile([P, G, N, 4], BF16, align_bytes=64)
         for half in range(2):
@@ -122,6 +121,7 @@ def tile_broadcastattention_w_kernel(tc, x, wq_words, wq_scales, bqkv, wp_words,
         bk_src = bqkv.rearrange("(g h r) -> g h r", g=G, r=R)
         for g in range(G):
             nc.scalar.dma_start(out=bk_col[:, g, 0:4], in_=bk_src[g, :, 1 : 1 + HD].rearrange("h (a t) -> h a t", t=4))
+        nc.scalar.dma_start(out=bpt[0:16, :], in_=bp.rearrange("(m p) -> m p", p=P))
 
         k_sb = keep.tile([P, 4, 4 * H], F32)
         v_sb = keep.tile([P, 4, 4 * H], F32)
@@ -251,50 +251,10 @@ def tile_broadcastattention_w_kernel(tc, x, wq_words, wq_scales, bqkv, wp_words,
                 in_=hg[:, r, :, :].rearrange("p n t -> p (n t)"),
             )
 
-        for kg in range(G):
-            passes(0, kg)
-        bps = ps_v.tile([P, 4, P], BF16, tag="v")
-        nc.tensor.transpose(out=bps[:, 0, :], in_=bpt[:], identity=ident_b[:])
-        bp_col = keep.tile([P, 16], F32)
-        nc.vector.tensor_copy(out=bp_col[:], in_=bps[:, 0, 0:16])
-        for r in range(G):
-            last = r == G - 1
-            for w in range(3):
-                q_copy(r, w)
-            for w in range(3):
-                v_evac(r, w)
-            for w in range(3):
-                k_copy(r, w)
-            passes(r + 1, 0)
-            transpose_q(r)
-            row_max(r)
-            exponent(r)
-            if r > 0:
-                transpose_s(r - 1)
-                transpose_v(r - 1)
-                product(r - 1)
-            if last:
-                transpose_v(r)
-            passes(r + 1, 1)
-            normalise(r)
-            passes(r + 1, 2)
-            if r > 0:
-                context(r - 1)
-                context_bias(r - 1)
-                if last:
-                    transpose_s(r)
-                    product(r)
-                hidden(r - 1)
-                quantise_h(r - 1)
-            passes(r + 1, 3)
-        context(G - 1)
-        context_bias(G - 1)
-        hidden(G - 1)
-        quantise_h(G - 1)
-
         out_sb = keep.tile([P, 16, N], F32)
         part_sb = keep.tile([P, 2 * SPLIT_PAIRS, N], F32)
         out_v = out[0].rearrange("(m p) n -> p m n", p=P)
+        bp_col = keep.tile([P, 16], F32)
 
         def stage2(dst, m, groups):
             for g in groups:
@@ -308,14 +268,15 @@ def tile_broadcastattention_w_kernel(tc, x, wq_words, wq_scales, bqkv, wp_words,
                     stop=(g == groups[-1]),
                 )
 
-        for j in range(SPLIT_PAIRS):
+        def first_part(j):
             pa = ps_w.tile([P, 2, N], F32, tag="w")
             for i in range(2):
                 stage2(pa[:, i, :], 2 * j + i, (0, 1, 2))
             for i in range(2):
                 m = 2 * j + i
                 nc.scalar.activation(out=part_sb[:, m, :], in_=pa[:, i, :], func=ACT.Identity, bias=bp_col[:, m : m + 1], scale=1.0)
-        for j in range(8):
+
+        def finish(j):
             po = ps_w.tile([P, 2, N], F32, tag="w")
             for i in range(2):
                 stage2(po[:, i, :], 2 * j + i, (3,) if j < SPLIT_PAIRS else (0, 1, 2, 3))
@@ -326,3 +287,52 @@ def tile_broadcastattention_w_kernel(tc, x, wq_words, wq_scales, bqkv, wp_words,
                     m = 2 * j + i
                     nc.scalar.activation(out=out_sb[:, m, :], in_=po[:, i, :], func=ACT.Identity, bias=bp_col[:, m : m + 1], scale=1.0)
             nc.sync.dma_start(out=out_v[:, 2 * j : 2 * j + 2, :], in_=out_sb[:, 2 * j : 2 * j + 2, :])
+
+        for kg in range(G):
+            passes(0, kg)
+        for r in range(G):
+            last = r == G - 1
+            for w in range(3):
+                q_copy(r, w)
+            for w in range(3):
+                v_evac(r, w)
+            for w in range(3):
+                k_copy(r, w)
+            passes(r + 1, 0)
+            transpose_q(r)
+            if r > 0:
+                context(r - 1)
+            if last:
+                transpose_v(r)
+            row_max(r)
+            exponent(r)
+            if r > 0:
+                context_bias(r - 1)
+                hidden(r - 1)
+            passes(r + 1, 1)
+            normalise(r)
+            if r > 0:
+                quantise_h(r - 1)
+            if r == 1:
+                bps = ps_v.tile([P, 4, P], BF16, tag="v")
+                nc.tensor.transpose(out=bps[:, 0, :], in_=bpt[:], identity=ident_b[:])
+                nc.vector.tensor_copy(out=bp_col[:], in_=bps[:, 0, 0:16])
+            passes(r + 1, 2)
+            transpose_s(r)
+            product(r)
+            passes(r + 1, 3)
+            if not last:
+                transpose_v(r)
+        first_part(0)
+        context(G - 1)
+        context_bias(G - 1)
+        hidden(G - 1)
+        quantise_h(G - 1)
+        for j in range(1, 6):
+            first_part(j)
+        for j in range(6):
+            finish(j)
+        for j in range(6, 8):
+            first_part(j)
+        for j in range(6, 8):
+            finish(j)

@@ -58,9 +58,10 @@ def tile_broadcastattention_w_kernel(tc, x, wq_words, wq_scales, bqkv, wp_words,
         ones_b = keep.tile([P, P], BF16)
         q_t = keep.tile([P, G, P], F32)
 
-        nc.vector.memset(pl[:].bitcast(I32), 0)
         nc.vector.memset(wp_pl[:].bitcast(I32), 0)
+        nc.vector.memset(pl[:].bitcast(I32), 0)
         nc.vector.memset(warm_in[:], 0.0)
+        nc.gpsimd.dma_start(out=xraw[:], in_=x[0].rearrange("(g p j) n -> p g (j n)", g=G, p=P, j=4))
         nc.gpsimd.memset(brow[:].bitcast(F32), 0.0)
         nc.gpsimd.dma_start(
             out=brow[0:1, :].rearrange("o (h d) -> o h d", d=HD),
@@ -70,21 +71,24 @@ def tile_broadcastattention_w_kernel(tc, x, wq_words, wq_scales, bqkv, wp_words,
         nc.gpsimd.memset(q_t[:], 0.0)
         make_identity(nc, ident_f[:])
         nc.gpsimd.memset(ones_f[:], 1.0)
+        bk_src = bqkv.rearrange("(g h r) -> g h r", g=G, r=R)
+        for g in range(G):
+            nc.gpsimd.dma_start(out=bk_col[:, g, 0:4], in_=bk_src[g, :, 1 : 1 + HD].rearrange("h (a t) -> h a t", t=4))
         nc.gpsimd.memset(bpt[:], 0.0)
+        nc.gpsimd.dma_start(out=bpt[0:16, :], in_=bp.rearrange("(m p) -> m p", p=P))
         make_identity(nc, ident_b[:])
 
-        nc.scalar.dma_start(out=xraw[:], in_=x[0].rearrange("(g p j) n -> p g (j n)", g=G, p=P, j=4))
         nc.scalar.activation(out=warm_out[:], in_=warm_in[:], func=ACT.Exp)
 
         for q in range(4):
             nc.sync.dma_start(
-                out=pl[32 * q : 32 * q + 16, :].bitcast(I32),
-                in_=wq_scales[:, 4 * q : 4 * q + 4, :].bitcast(I32),
+                out=wp_pl[32 * q : 32 * q + 16, :].bitcast(I32),
+                in_=wp_scales[:, 4 * q : 4 * q + 4, :].bitcast(I32),
             )
         for q in range(4):
             nc.sync.dma_start(
-                out=wp_pl[32 * q : 32 * q + 16, :].bitcast(I32),
-                in_=wp_scales[:, 4 * q : 4 * q + 4, :].bitcast(I32),
+                out=pl[32 * q : 32 * q + 16, :].bitcast(I32),
+                in_=wq_scales[:, 4 * q : 4 * q + 4, :].bitcast(I32),
             )
         wq_src = wq_words.rearrange("g p n t -> p g (n t)")
         for r in range(G):
@@ -118,10 +122,6 @@ def tile_broadcastattention_w_kernel(tc, x, wq_words, wq_scales, bqkv, wp_words,
             pb = ps_w.tile([P, 512], F32, tag="w")
             nc.tensor.matmul(out=pb[:], lhsT=ones_b[:], rhs=brow[:, 512 * j : 512 * (j + 1)], start=True, stop=True)
             nc.scalar.copy(out=bias_v[:, 32 * j : 32 * (j + 1), :].rearrange("p h d -> p (h d)"), in_=pb[:])
-        bk_src = bqkv.rearrange("(g h r) -> g h r", g=G, r=R)
-        for g in range(G):
-            nc.scalar.dma_start(out=bk_col[:, g, 0:4], in_=bk_src[g, :, 1 : 1 + HD].rearrange("h (a t) -> h a t", t=4))
-        nc.scalar.dma_start(out=bpt[0:16, :], in_=bp.rearrange("(m p) -> m p", p=P))
 
         k_sb = keep.tile([P, 4, 4 * H], F32)
         v_sb = keep.tile([P, 4, 4 * H], F32)
@@ -313,7 +313,7 @@ def tile_broadcastattention_w_kernel(tc, x, wq_words, wq_scales, bqkv, wp_words,
             normalise(r)
             if r > 0:
                 quantise_h(r - 1)
-            if r == 1:
+            if r == 2:
                 bps = ps_v.tile([P, 4, P], BF16, tag="v")
                 nc.tensor.transpose(out=bps[:, 0, :], in_=bpt[:], identity=ident_b[:])
                 nc.vector.tensor_copy(out=bp_col[:], in_=bps[:, 0, 0:16])

@@ -26,6 +26,7 @@ RC = HR * R
 WINDOWS = ((0, 512, 0, 15), (480, 512, 15, 30), (928, 128, 30, 32))
 WP_CHUNKS = ((0, 1024, 0, 4), (1024, 1536, 0, 4), (1536, 2048, 0, 3), (1536, 2048, 3, 4))
 SPLIT_PAIRS = 8
+VECTOR_PARTS = (0, 1, 6)
 
 FLOPS = 2 * O * DIM * N + 2 * DIM * DIM * N
 
@@ -58,10 +59,9 @@ def tile_broadcastattention_w_kernel(tc, x, wq_words, wq_scales, bqkv, wp_words,
         ones_b = keep.tile([P, P], BF16)
         q_t = keep.tile([P, G, P], F32)
 
-        nc.vector.memset(wp_pl[:].bitcast(I32), 0)
         nc.vector.memset(pl[:].bitcast(I32), 0)
+        nc.vector.memset(wp_pl[:].bitcast(I32), 0)
         nc.vector.memset(warm_in[:], 0.0)
-        nc.gpsimd.dma_start(out=xraw[:], in_=x[0].rearrange("(g p j) n -> p g (j n)", g=G, p=P, j=4))
         nc.gpsimd.memset(brow[:].bitcast(F32), 0.0)
         nc.gpsimd.dma_start(
             out=brow[0:1, :].rearrange("o (h d) -> o h d", d=HD),
@@ -71,24 +71,21 @@ def tile_broadcastattention_w_kernel(tc, x, wq_words, wq_scales, bqkv, wp_words,
         nc.gpsimd.memset(q_t[:], 0.0)
         make_identity(nc, ident_f[:])
         nc.gpsimd.memset(ones_f[:], 1.0)
-        bk_src = bqkv.rearrange("(g h r) -> g h r", g=G, r=R)
-        for g in range(G):
-            nc.gpsimd.dma_start(out=bk_col[:, g, 0:4], in_=bk_src[g, :, 1 : 1 + HD].rearrange("h (a t) -> h a t", t=4))
         nc.gpsimd.memset(bpt[:], 0.0)
-        nc.gpsimd.dma_start(out=bpt[0:16, :], in_=bp.rearrange("(m p) -> m p", p=P))
         make_identity(nc, ident_b[:])
 
+        nc.scalar.dma_start(out=xraw[:], in_=x[0].rearrange("(g p j) n -> p g (j n)", g=G, p=P, j=4))
         nc.scalar.activation(out=warm_out[:], in_=warm_in[:], func=ACT.Exp)
 
         for q in range(4):
             nc.sync.dma_start(
-                out=wp_pl[32 * q : 32 * q + 16, :].bitcast(I32),
-                in_=wp_scales[:, 4 * q : 4 * q + 4, :].bitcast(I32),
+                out=pl[32 * q : 32 * q + 16, :].bitcast(I32),
+                in_=wq_scales[:, 4 * q : 4 * q + 4, :].bitcast(I32),
             )
         for q in range(4):
             nc.sync.dma_start(
-                out=pl[32 * q : 32 * q + 16, :].bitcast(I32),
-                in_=wq_scales[:, 4 * q : 4 * q + 4, :].bitcast(I32),
+                out=wp_pl[32 * q : 32 * q + 16, :].bitcast(I32),
+                in_=wp_scales[:, 4 * q : 4 * q + 4, :].bitcast(I32),
             )
         wq_src = wq_words.rearrange("g p n t -> p g (n t)")
         for r in range(G):
@@ -122,6 +119,10 @@ def tile_broadcastattention_w_kernel(tc, x, wq_words, wq_scales, bqkv, wp_words,
             pb = ps_w.tile([P, 512], F32, tag="w")
             nc.tensor.matmul(out=pb[:], lhsT=ones_b[:], rhs=brow[:, 512 * j : 512 * (j + 1)], start=True, stop=True)
             nc.scalar.copy(out=bias_v[:, 32 * j : 32 * (j + 1), :].rearrange("p h d -> p (h d)"), in_=pb[:])
+        bk_src = bqkv.rearrange("(g h r) -> g h r", g=G, r=R)
+        for g in range(G):
+            nc.scalar.dma_start(out=bk_col[:, g, 0:4], in_=bk_src[g, :, 1 : 1 + HD].rearrange("h (a t) -> h a t", t=4))
+        nc.scalar.dma_start(out=bpt[0:16, :], in_=bp.rearrange("(m p) -> m p", p=P))
 
         k_sb = keep.tile([P, 4, 4 * H], F32)
         v_sb = keep.tile([P, 4, 4 * H], F32)
@@ -272,9 +273,17 @@ def tile_broadcastattention_w_kernel(tc, x, wq_words, wq_scales, bqkv, wp_words,
             pa = ps_w.tile([P, 2, N], F32, tag="w")
             for i in range(2):
                 stage2(pa[:, i, :], 2 * j + i, (0, 1, 2))
-            for i in range(2):
-                m = 2 * j + i
-                nc.scalar.activation(out=part_sb[:, m, :], in_=pa[:, i, :], func=ACT.Identity, bias=bp_col[:, m : m + 1], scale=1.0)
+            if j in VECTOR_PARTS:
+                nc.vector.tensor_tensor(
+                    out=part_sb[:, 2 * j : 2 * j + 2, :],
+                    in0=pa[:],
+                    in1=bp_col[:, 2 * j : 2 * j + 2].unsqueeze(2).to_broadcast([P, 2, N]),
+                    op=ALU.add,
+                )
+            else:
+                for i in range(2):
+                    m = 2 * j + i
+                    nc.scalar.activation(out=part_sb[:, m, :], in_=pa[:, i, :], func=ACT.Identity, bias=bp_col[:, m : m + 1], scale=1.0)
 
         def finish(j):
             po = ps_w.tile([P, 2, N], F32, tag="w")
@@ -313,7 +322,7 @@ def tile_broadcastattention_w_kernel(tc, x, wq_words, wq_scales, bqkv, wp_words,
             normalise(r)
             if r > 0:
                 quantise_h(r - 1)
-            if r == 2:
+            if r == 1:
                 bps = ps_v.tile([P, 4, P], BF16, tag="v")
                 nc.tensor.transpose(out=bps[:, 0, :], in_=bpt[:], identity=ident_b[:])
                 nc.vector.tensor_copy(out=bp_col[:], in_=bps[:, 0, 0:16])
@@ -324,11 +333,12 @@ def tile_broadcastattention_w_kernel(tc, x, wq_words, wq_scales, bqkv, wp_words,
             if not last:
                 transpose_v(r)
         first_part(0)
+        first_part(1)
         context(G - 1)
         context_bias(G - 1)
         hidden(G - 1)
         quantise_h(G - 1)
-        for j in range(1, 6):
+        for j in range(2, 6):
             first_part(j)
         for j in range(6):
             finish(j)

@@ -25,8 +25,6 @@ HR = H // G
 RC = HR * R
 WINDOWS = ((0, 512, 0, 15), (480, 512, 15, 30), (928, 128, 30, 32))
 WP_CHUNKS = ((0, 1024, 0, 4), (1024, 1536, 0, 4), (1536, 2048, 0, 3), (1536, 2048, 3, 4))
-SPLIT_PAIRS = 8
-VECTOR_PARTS = (0, 1, 6)
 
 FLOPS = 2 * O * DIM * N + 2 * DIM * DIM * N
 
@@ -37,55 +35,44 @@ def tile_broadcastattention_w_kernel(tc, x, wq_words, wq_scales, bqkv, wp_words,
         ctx.enter_context(tc.manual_schedule())
         keep = ctx.enter_context(tc.tile_pool(name="keep", bufs=1))
         work = ctx.enter_context(tc.tile_pool(name="work", bufs=2))
-        ps_w = ctx.enter_context(tc.psum_pool(name="ps_w", bufs=4))
-        ps_c = ctx.enter_context(tc.psum_pool(name="ps_c", bufs=1))
-        ps_s = ctx.enter_context(tc.psum_pool(name="ps_s", bufs=2))
-        ps_v = ctx.enter_context(tc.psum_pool(name="ps_v", bufs=1))
+        psum = ctx.enter_context(tc.psum_pool(name="psum", bufs=1))
+
+        def bank(i):
+            return psum.tile([P, 512], F32, tag="b%d" % i, name="bank")
 
         pl = keep.tile([P, O], U8, align_bytes=64)
         pl2 = keep.tile([P, O + 64], U8, align_bytes=64)
+        q_pl = keep.tile([P, 4 * H], U8, align_bytes=64)
         wp_pl = keep.tile([P, DIM], U8, align_bytes=64)
         wq = keep.tile([P, G, O], U32, align_bytes=64)
+        q_w = keep.tile([P, G, G, 4 * HR], U32, align_bytes=64)
         wp = keep.tile([P, G, DIM], U32, align_bytes=64)
         xraw = keep.tile([P, G, 4 * N], BF16)
-        brow = keep.tile([P, H * HD], BF16)
+        bq = keep.tile([P, R], BF16)
         bpt = keep.tile([P, P], BF16)
-        bk_col = keep.tile([P, G, 16], BF16)
         warm_in = keep.tile([P, 1], F32)
+        dummy = keep.tile([P, 512], BF16)
         warm_out = keep.tile([P, 1], F32)
         ident_f = keep.tile([P, P], F32)
         ident_b = keep.tile([P, P], BF16)
-        ones_f = keep.tile([P, 2], F32)
-        ones_b = keep.tile([P, P], BF16)
-        q_t = keep.tile([P, G, P], F32)
 
+        nc.vector.memset(warm_in[:], 0.0)
+        nc.vector.memset(dummy[:].bitcast(F32), 0.0)
         nc.vector.memset(pl[:].bitcast(I32), 0)
         nc.vector.memset(wp_pl[:].bitcast(I32), 0)
-        nc.vector.memset(warm_in[:], 0.0)
-        nc.gpsimd.memset(brow[:].bitcast(F32), 0.0)
-        nc.gpsimd.dma_start(
-            out=brow[0:1, :].rearrange("o (h d) -> o h d", d=HD),
-            in_=bqkv.rearrange("(o h r) -> o h r", o=1, r=R)[:, :, 1 + HD : R],
-        )
-        nc.gpsimd.memset(ones_b[:], 1.0)
-        nc.gpsimd.memset(q_t[:], 0.0)
-        make_identity(nc, ident_f[:])
-        nc.gpsimd.memset(ones_f[:], 1.0)
-        nc.gpsimd.memset(bpt[:], 0.0)
-        make_identity(nc, ident_b[:])
-
-        nc.scalar.dma_start(out=xraw[:], in_=x[0].rearrange("(g p j) n -> p g (j n)", g=G, p=P, j=4))
         nc.scalar.activation(out=warm_out[:], in_=warm_in[:], func=ACT.Exp)
 
+        nc.gpsimd.dma_start(out=bq[:], in_=bqkv.rearrange("(h r) -> h r", r=R))
+        nc.gpsimd.memset(bpt[:], 0.0)
+        nc.gpsimd.dma_start(out=bpt[0:16, :], in_=bp.rearrange("(m p) -> m p", p=P))
+        make_identity(nc, ident_b[:])
+        make_identity(nc, ident_f[:])
+
+        nc.sync.dma_start(out=xraw[:], in_=x[0].rearrange("(g p j) n -> p g (j n)", g=G, p=P, j=4))
         for q in range(4):
             nc.sync.dma_start(
                 out=pl[32 * q : 32 * q + 16, :].bitcast(I32),
                 in_=wq_scales[:, 4 * q : 4 * q + 4, :].bitcast(I32),
-            )
-        for q in range(4):
-            nc.sync.dma_start(
-                out=wp_pl[32 * q : 32 * q + 16, :].bitcast(I32),
-                in_=wp_scales[:, 4 * q : 4 * q + 4, :].bitcast(I32),
             )
         wq_src = wq_words.rearrange("g p n t -> p g (n t)")
         for r in range(G):
@@ -94,6 +81,11 @@ def tile_broadcastattention_w_kernel(tc, x, wq_words, wq_scales, bqkv, wp_words,
                     out=wq[:, kg, RC * r : RC * (r + 1)].bitcast(I32),
                     in_=wq_src[:, kg, 4 * RC * r : 4 * RC * (r + 1)].bitcast(I32),
                 )
+        for q in range(4):
+            nc.sync.dma_start(
+                out=wp_pl[32 * q : 32 * q + 16, :].bitcast(I32),
+                in_=wp_scales[:, 4 * q : 4 * q + 4, :].bitcast(I32),
+            )
         wp_src = wp_words.rearrange("g p n t -> p g (n t)")
         for c0, c1, g0, g1 in WP_CHUNKS:
             nc.sync.dma_start(out=wp[:, g0:g1, c0:c1].bitcast(I32), in_=wp_src[:, g0:g1, 4 * c0 : 4 * c1].bitcast(I32))
@@ -112,17 +104,35 @@ def tile_broadcastattention_w_kernel(tc, x, wq_words, wq_scales, bqkv, wp_words,
                 scales=xs[:, 2 * N * half : 2 * N * (half + 1)],
                 in_=xg[:, 2 * half : 2 * half + 2, :, :].rearrange("p g n j -> p (g n j)"),
             )
-        nc.vector.tensor_copy(out=pl2[:].bitcast(I32)[:, 8 : 8 + O // 4], in_=pl[:].bitcast(I32))
 
-        bias_v = keep.tile([P, H, HD], BF16)
-        for j in range(4):
-            pb = ps_w.tile([P, 512], F32, tag="w")
-            nc.tensor.matmul(out=pb[:], lhsT=ones_b[:], rhs=brow[:, 512 * j : 512 * (j + 1)], start=True, stop=True)
-            nc.scalar.copy(out=bias_v[:, 32 * j : 32 * (j + 1), :].rearrange("p h d -> p (h d)"), in_=pb[:])
-        bk_src = bqkv.rearrange("(g h r) -> g h r", g=G, r=R)
-        for g in range(G):
-            nc.scalar.dma_start(out=bk_col[:, g, 0:4], in_=bk_src[g, :, 1 : 1 + HD].rearrange("h (a t) -> h a t", t=4))
-        nc.scalar.dma_start(out=bpt[0:16, :], in_=bp.rearrange("(m p) -> m p", p=P))
+        sel = keep.tile([P, 4 * H], BF16)
+        nc.vector.tensor_copy(out=sel[:].rearrange("p (h a) -> p h a", a=4), in_=ident_b[:].unsqueeze(2).to_broadcast([P, H, 4]))
+        mask = keep.tile([P, 4], F32)
+        nc.vector.tensor_reduce(out=mask[:], in_=ident_f[:].rearrange("p (h a) -> p a h", a=4), axis=AX.X, op=ALU.add)
+        bias_ps = bank(5)
+
+        def warm_up(count):
+            for i in range(count):
+                nc.tensor.matmul(out=bank(i % 4)[:], lhsT=dummy[:, 0:P], rhs=dummy[:], start=True, stop=True)
+
+        warm_up(8)
+        for r in range(G):
+            nc.tensor.matmul(out=bias_ps[:, 32 * r : 32 * (r + 1)], lhsT=sel[:, P * r : P * (r + 1)], rhs=bq[:, 1:R], start=True, stop=True)
+        warm_up(4)
+        nc.vector.tensor_copy(out=pl2[:].bitcast(I32)[:, 8 : 8 + O // 4], in_=pl[:].bitcast(I32))
+        for a in range(4):
+            nc.vector.tensor_copy(out=q_pl[:, a : 4 * H : 4], in_=pl[:, 0 : O : R])
+
+        masked = keep.tile([P, 8, 4, 4], F32)
+        bias_kv = keep.tile([P, 8, 4], F32)
+        bias_p = keep.tile([P, 16], F32)
+        nc.vector.tensor_tensor(
+            out=masked[:],
+            in0=bias_ps[:, 0:P].rearrange("p (q a t) -> p q a t", a=4, t=4),
+            in1=mask[:].unsqueeze(1).unsqueeze(3).to_broadcast([P, 8, 4, 4]),
+            op=ALU.mult,
+        )
+        nc.vector.tensor_reduce(out=bias_kv[:], in_=masked[:].rearrange("p q a t -> p q t a"), axis=AX.X, op=ALU.add)
 
         k_sb = keep.tile([P, 4, 4 * H], F32)
         v_sb = keep.tile([P, 4, 4 * H], F32)
@@ -130,12 +140,12 @@ def tile_broadcastattention_w_kernel(tc, x, wq_words, wq_scales, bqkv, wp_words,
         hw = keep.tile([P, G * N], U32, align_bytes=64)
         hs = keep.tile([P, G * N], U8, align_bytes=64)
         win = {}
+        tl = {}
 
         def one_pass(r, w, kg):
             c, width, h0, h1 = WINDOWS[w]
             if kg == 0:
-                pool, tag = (ps_w, "w") if w < 2 else (ps_c, "c")
-                win[(r, w)] = pool.tile([P, 512], F32, tag=tag, name="win")
+                win[(r, w)] = bank(2 * (r % 2) + w if w < 2 else 4)
             col = RC * r + c
             plane, pc = (pl, col) if col % 64 == 0 else (pl2, col + 32)
             nc.tensor.matmul_mx(
@@ -148,101 +158,92 @@ def tile_broadcastattention_w_kernel(tc, x, wq_words, wq_scales, bqkv, wp_words,
                 stop=(kg == G - 1),
             )
 
+        def q_words(r, kg):
+            src = wq[:, kg, RC * r : RC * (r + 1) : R].bitcast(I32)
+            (nc.vector if kg == G - 1 else nc.gpsimd).tensor_copy(
+                out=q_w[:, r, kg, :].bitcast(I32).rearrange("p (h a) -> p h a", a=4),
+                in_=src.unsqueeze(2).to_broadcast([P, HR, 4]),
+            )
+
+        def q_passes(r):
+            tl[("tq", r)] = bank(6)[:, 0:P]
+            for kg in range(G):
+                nc.tensor.matmul_mx(
+                    out=tl[("tq", r)],
+                    lhsT=q_w[:, r, kg, :].bitcast(FP8X4),
+                    lhsT_scale=q_pl[4 * kg : P, P * r : P * (r + 1)],
+                    rhs=xw[:, N * kg : N * (kg + 1)].bitcast(FP8X4),
+                    rhs_scale=xs[:, N * kg : N * (kg + 1)],
+                    start=(kg == 0),
+                    stop=(kg == G - 1),
+                )
+
         def passes(r, kg):
             if r < G:
-                if kg == G - 1:
-                    for early in range(G - 1):
-                        one_pass(r, 2, early)
+                if kg < G - 1:
+                    q_words(r, kg)
                 one_pass(r, 0, kg)
+                if kg == G - 1:
+                    q_passes(r)
                 one_pass(r, 1, kg)
                 if kg == G - 1:
-                    one_pass(r, 2, kg)
+                    for each in range(G):
+                        one_pass(r, 2, each)
 
-        def heads(r, w):
+        def evacuate(copy, dst, part, r, w):
             c, width, h0, h1 = WINDOWS[w]
             off = R * h0 - c
-            return win[(r, w)][:, off : off + R * (h1 - h0)].rearrange("p (h r) -> p h r", r=R)
-
-        def q_copy(r, w):
-            c, width, h0, h1 = WINDOWS[w]
-            nc.scalar.copy(out=q_t[:, r, h0:h1], in_=heads(r, w)[:, :, 0])
-
-        def k_copy(r, w):
-            c, width, h0, h1 = WINDOWS[w]
-            nc.scalar.copy(
-                out=k_sb[:, :, 4 * (HR * r + h0) : 4 * (HR * r + h1)].rearrange("p t (h a) -> p t h a", a=4),
-                in_=heads(r, w)[:, :, 1 : 1 + HD].rearrange("p h (a t) -> p t h a", t=4),
+            heads = win[(r, w)][:, off : off + R * (h1 - h0)].rearrange("p (h r) -> p h r", r=R)
+            copy(
+                out=dst[:, :, 4 * (HR * r + h0) : 4 * (HR * r + h1)].rearrange("p t (h a) -> p t h a", a=4),
+                in_=heads[:, :, 1 + HD * part : 1 + HD * (part + 1)].rearrange("p h (a t) -> p t h a", t=4),
             )
-
-        def v_evac(r, w):
-            c, width, h0, h1 = WINDOWS[w]
-            nc.vector.tensor_tensor(
-                out=v_sb[:, :, 4 * (HR * r + h0) : 4 * (HR * r + h1)].rearrange("p t (h a) -> p t h a", a=4),
-                in0=heads(r, w)[:, :, 1 + HD : R].rearrange("p h (a t) -> p t h a", t=4),
-                in1=bias_v[:, HR * r + h0 : HR * r + h1, :].rearrange("p h (a t) -> p t h a", t=4),
-                op=ALU.add,
-            )
-
-        tl = {}
-
-        def transpose_q(r):
-            small = ps_s.tile([P, 512], F32, tag="s")
-            tl[("tq", r)] = small[:, 0:P]
-            tl[("st", r)] = small[:, P : 2 * P]
-            tl[("cx", r)] = small[:, 2 * P : 2 * P + 8].rearrange("p (t two) -> p t two", two=2)
-            nc.tensor.transpose(out=tl[("tq", r)], in_=q_t[:, r, :], identity=ident_f[:])
 
         def row_max(r):
             tl[("negmax", r)] = work.tile([P, 1], F32, tag="negmax", name="negmax")
             nc.vector.tensor_reduce(out=tl[("negmax", r)][:], in_=tl[("tq", r)], axis=AX.X, op=ALU.max, negate=True)
 
         def exponent(r):
-            tl[("e", r)] = work.tile([P, P], F32, tag="e", name="e_sb")
+            tl[("e", r)] = work.tile([P, N], F32, tag="e", name="e_sb")
             tl[("esum", r)] = work.tile([P, 1], F32, tag="esum", name="esum")
             nc.scalar.activation(
                 out=tl[("e", r)][:], in_=tl[("tq", r)], func=ACT.Exp, bias=tl[("negmax", r)][:, 0:1], scale=1.0, accum_out=tl[("esum", r)][:]
             )
 
-        def normalise(r):
-            rsum = work.tile([P, 1], F32, tag="rsum")
-            nc.vector.reciprocal(out=rsum[:], in_=tl[("esum", r)][:])
-            tl[("s", r)] = work.tile([P, P], F32, tag="s_sb", name="s_sb")
-            nc.vector.tensor_scalar_mul(out=tl[("s", r)][:], in0=tl[("e", r)][:], scalar1=rsum[:, 0:1])
+        def inverse_sum(r):
+            tl[("rsum", r)] = work.tile([P, 1], F32, tag="rsum", name="rsum")
+            nc.vector.reciprocal(out=tl[("rsum", r)][:], in_=tl[("esum", r)][:])
 
-        def transpose_s(r):
-            nc.tensor.transpose(out=tl[("st", r)], in_=tl[("s", r)][:], identity=ident_f[:])
-
-        def transpose_v(r):
-            pool, tag = (ps_v, "v") if r < G - 1 else (ps_c, "c")
-            tl[("vps", r)] = pool.tile([P, 4, P], F32, tag=tag, name="vps")
+        def transpose(key, b, src, r):
+            tl[(key, r)] = bank(b)[:].rearrange("p (t n) -> p t n", t=4)
             for t in range(4):
-                nc.tensor.transpose(out=tl[("vps", r)][:, t, :], in_=v_sb[:, t, P * r : P * (r + 1)], identity=ident_f[:])
-
-        def product(r):
-            tl[("prod", r)] = work.tile([P, 4, P], F32, tag="prod", name="prod")
-            nc.vector.tensor_tensor(
-                out=tl[("prod", r)][:].rearrange("p t (h a) -> p t h a", a=4),
-                in0=k_sb[:, :, P * r : P * (r + 1)].rearrange("p t (h a) -> p t h a", a=4),
-                in1=tl[("st", r)][:, 0:HR].unsqueeze(1).unsqueeze(3).to_broadcast([P, 4, HR, 4]),
-                op=ALU.mult,
-            )
+                nc.tensor.transpose(out=tl[(key, r)][:, t, :], in_=src[:, t, P * r : P * (r + 1)], identity=ident_f[:])
 
         def context(r):
+            acc = work.tile([P, 4], F32, tag="acc")
+            product = work.tile([P, N], F32, tag="product")
             for t in range(4):
-                nc.tensor.matmul(out=tl[("cx", r)][:, t, :], lhsT=tl[("prod", r)][:, t, :], rhs=ones_f[:], start=True, stop=True)
-
-        def context_bias(r):
+                nc.vector.scalar_tensor_tensor(
+                    out=product[:], in0=tl[("k", r)][:, t, :], scalar=1.0, in1=tl[("e", r)][:], op0=ALU.mult, op1=ALU.mult, accum_out=acc[:, t : t + 1]
+                )
             tl[("ctx", r)] = work.tile([P, 4], F32, tag="ctx", name="ctx_sb")
-            nc.vector.tensor_tensor(out=tl[("ctx", r)][:], in0=tl[("cx", r)][:, :, 0], in1=bk_col[:, r, 0:4], op=ALU.add)
+            nc.vector.scalar_tensor_tensor(
+                out=tl[("ctx", r)][:], in0=acc[:], scalar=tl[("rsum", r)][:, 0:1], in1=bias_kv[:, 2 * r, :], op0=ALU.mult, op1=ALU.add
+            )
+
+        def relu(r):
+            tl[("relu", r)] = work.tile([P, 4, N], F32, tag="relu", name="relu_v")
+            for t in range(4):
+                nc.scalar.activation(
+                    out=tl[("relu", r)][:, t, :], in_=tl[("v", r)][:, t, :], func=ACT.Relu, bias=bias_kv[:, 2 * r + 1, t : t + 1], scale=1.0
+                )
 
         def hidden(r):
-            nc.vector.scalar_tensor_tensor(
+            nc.vector.tensor_tensor(
                 out=hg[:, r, :, :],
-                in0=tl[("vps", r)][:].rearrange("p t n -> p n t"),
-                scalar=0.0,
+                in0=tl[("relu", r)][:].rearrange("p t n -> p n t"),
                 in1=tl[("ctx", r)][:].unsqueeze(1).to_broadcast([P, N, 4]),
-                op0=ALU.max,
-                op1=ALU.mult,
+                op=ALU.mult,
             )
 
         def quantise_h(r):
@@ -253,9 +254,7 @@ def tile_broadcastattention_w_kernel(tc, x, wq_words, wq_scales, bqkv, wp_words,
             )
 
         out_sb = keep.tile([P, 16, N], F32)
-        part_sb = keep.tile([P, 2 * SPLIT_PAIRS, N], F32)
         out_v = out[0].rearrange("(m p) n -> p m n", p=P)
-        bp_col = keep.tile([P, 16], F32)
 
         def stage2(dst, m, groups):
             for g in groups:
@@ -265,84 +264,73 @@ def tile_broadcastattention_w_kernel(tc, x, wq_words, wq_scales, bqkv, wp_words,
                     lhsT_scale=wp_pl[4 * g : P, P * m : P * (m + 1)],
                     rhs=hw[:, N * g : N * (g + 1)].bitcast(FP8X4),
                     rhs_scale=hs[:, N * g : N * (g + 1)],
-                    start=(g == groups[0]),
-                    stop=(g == groups[-1]),
+                    start=(g == 0),
+                    stop=(g == G - 1),
                 )
 
-        def first_part(j):
-            pa = ps_w.tile([P, 2, N], F32, tag="w")
-            for i in range(2):
-                stage2(pa[:, i, :], 2 * j + i, (0, 1, 2))
-            if j in VECTOR_PARTS:
-                nc.vector.tensor_tensor(
-                    out=part_sb[:, 2 * j : 2 * j + 2, :],
-                    in0=pa[:],
-                    in1=bp_col[:, 2 * j : 2 * j + 2].unsqueeze(2).to_broadcast([P, 2, N]),
-                    op=ALU.add,
-                )
-            else:
-                for i in range(2):
-                    m = 2 * j + i
-                    nc.scalar.activation(out=part_sb[:, m, :], in_=pa[:, i, :], func=ACT.Identity, bias=bp_col[:, m : m + 1], scale=1.0)
+        def out_scalar(m, src):
+            nc.scalar.activation(out=out_sb[:, m, :], in_=src, func=ACT.Identity, bias=bias_p[:, m : m + 1], scale=1.0)
 
-        def finish(j):
-            po = ps_w.tile([P, 2, N], F32, tag="w")
-            for i in range(2):
-                stage2(po[:, i, :], 2 * j + i, (3,) if j < SPLIT_PAIRS else (0, 1, 2, 3))
-            if j < SPLIT_PAIRS:
-                nc.vector.tensor_tensor(out=out_sb[:, 2 * j : 2 * j + 2, :], in0=po[:], in1=part_sb[:, 2 * j : 2 * j + 2, :], op=ALU.add)
-            else:
-                for i in range(2):
-                    m = 2 * j + i
-                    nc.scalar.activation(out=out_sb[:, m, :], in_=po[:, i, :], func=ACT.Identity, bias=bp_col[:, m : m + 1], scale=1.0)
-            nc.sync.dma_start(out=out_v[:, 2 * j : 2 * j + 2, :], in_=out_sb[:, 2 * j : 2 * j + 2, :])
+        def out_vector(m, src):
+            nc.vector.tensor_scalar_add(out=out_sb[:, m, :], in0=src, scalar1=bias_p[:, m : m + 1])
 
-        for kg in range(G):
+        def store(m):
+            nc.sync.dma_start(out=out_v[:, m : m + 2, :], in_=out_sb[:, m : m + 2, :])
+
+        for kg in range(G - 1):
             passes(0, kg)
         for r in range(G):
-            last = r == G - 1
-            for w in range(3):
-                q_copy(r, w)
-            for w in range(3):
-                v_evac(r, w)
-            for w in range(3):
-                k_copy(r, w)
-            passes(r + 1, 0)
-            transpose_q(r)
-            if r > 0:
-                context(r - 1)
-            if last:
-                transpose_v(r)
-            row_max(r)
-            exponent(r)
-            if r > 0:
-                context_bias(r - 1)
+            if r == G - 1:
                 hidden(r - 1)
-            passes(r + 1, 1)
-            normalise(r)
-            if r > 0:
                 quantise_h(r - 1)
+            q_words(r, G - 1)
+            passes(r, G - 1)
+            if 0 < r < G - 1:
+                hidden(r - 1)
+            evacuate(nc.vector.tensor_copy, k_sb, 0, r, 0)
+            row_max(r)
+            if 0 < r < G - 1:
+                quantise_h(r - 1)
+            evacuate(nc.scalar.copy, k_sb, 0, r, 1)
+            evacuate(nc.scalar.copy, k_sb, 0, r, 2)
+            exponent(r)
+            for w in range(3):
+                evacuate(nc.vector.tensor_copy, v_sb, 1, r, w)
+            passes(r + 1, 0)
+            transpose("k", 5, k_sb, r)
+            transpose("v", 7, v_sb, r)
+            passes(r + 1, 1)
+            inverse_sum(r)
+            context(r)
+            relu(r)
             if r == 1:
-                bps = ps_v.tile([P, 4, P], BF16, tag="v")
-                nc.tensor.transpose(out=bps[:, 0, :], in_=bpt[:], identity=ident_b[:])
-                nc.vector.tensor_copy(out=bp_col[:], in_=bps[:, 0, 0:16])
+                bp_ps = bank(5)
+                nc.tensor.matmul(out=bp_ps[:, 0:16], lhsT=bpt[:], rhs=ident_b[:, 0:16], start=True, stop=True)
+                nc.scalar.copy(out=bias_p[:], in_=bp_ps[:, 0:16])
             passes(r + 1, 2)
-            transpose_s(r)
-            product(r)
-            passes(r + 1, 3)
-            if not last:
-                transpose_v(r)
-        first_part(0)
-        first_part(1)
-        context(G - 1)
-        context_bias(G - 1)
+        first = [bank(b)[:, 0:N] for b in range(4)]
+        for m in range(4):
+            stage2(first[m], m, range(3))
         hidden(G - 1)
         quantise_h(G - 1)
+        for m in range(4):
+            stage2(first[m], m, range(3, 4))
+            (out_vector if m % 2 else out_scalar)(m, first[m])
+        store(0)
+        store(2)
         for j in range(2, 6):
-            first_part(j)
-        for j in range(6):
-            finish(j)
-        for j in range(6, 8):
-            first_part(j)
-        for j in range(6, 8):
-            finish(j)
+            po = bank(2 + j)
+            for i in range(2):
+                stage2(po[:, N * i : N * (i + 1)], 2 * j + i, range(G))
+            for i in range(2):
+                (out_vector if j % 2 else out_scalar)(2 * j + i, po[:, N * i : N * (i + 1)])
+            store(2 * j)
+        last = [bank(b)[:, 0:N] for b in range(4)]
+        for i in range(4):
+            stage2(last[i], 12 + i, range(3))
+        for i in range(4):
+            stage2(last[i], 12 + i, range(3, 4))
+        for i in range(4):
+            (out_vector if i % 2 else out_scalar)(12 + i, last[i])
+        store(12)
+        store(14)

@@ -57,8 +57,8 @@ def tile_broadcastattention_w_kernel(tc, x, wq_words, wq_scales, bqkv, wp_words,
         ident_b = keep.tile([P, P], BF16)
 
         nc.vector.memset(warm_in[:], 0.0)
-        nc.vector.memset(dummy[:].bitcast(F32), 0.0)
         nc.vector.memset(pl[:].bitcast(I32), 0)
+        nc.vector.memset(dummy[:].bitcast(F32), 0.0)
         nc.vector.memset(wp_pl[:].bitcast(I32), 0)
         nc.scalar.activation(out=warm_out[:], in_=warm_in[:], func=ACT.Exp)
 
@@ -160,7 +160,7 @@ def tile_broadcastattention_w_kernel(tc, x, wq_words, wq_scales, bqkv, wp_words,
 
         def q_words(r, kg):
             src = wq[:, kg, RC * r : RC * (r + 1) : R].bitcast(I32)
-            (nc.vector if kg == G - 1 else nc.gpsimd).tensor_copy(
+            (nc.vector if kg == r == G - 1 else nc.gpsimd).tensor_copy(
                 out=q_w[:, r, kg, :].bitcast(I32).rearrange("p (h a) -> p h a", a=4),
                 in_=src.unsqueeze(2).to_broadcast([P, HR, 4]),
             )
@@ -274,32 +274,28 @@ def tile_broadcastattention_w_kernel(tc, x, wq_words, wq_scales, bqkv, wp_words,
         def out_vector(m, src):
             nc.vector.tensor_scalar_add(out=out_sb[:, m, :], in0=src, scalar1=bias_p[:, m : m + 1])
 
-        def store(m):
-            nc.sync.dma_start(out=out_v[:, m : m + 2, :], in_=out_sb[:, m : m + 2, :])
+        def store(m0, m1):
+            nc.sync.dma_start(out=out_v[:, m0:m1, :], in_=out_sb[:, m0:m1, :])
 
         for kg in range(G - 1):
             passes(0, kg)
         for r in range(G):
-            if r == G - 1:
-                hidden(r - 1)
-                quantise_h(r - 1)
             q_words(r, G - 1)
             passes(r, G - 1)
-            if 0 < r < G - 1:
-                hidden(r - 1)
             evacuate(nc.vector.tensor_copy, k_sb, 0, r, 0)
             row_max(r)
-            if 0 < r < G - 1:
+            if r > 0:
+                hidden(r - 1)
                 quantise_h(r - 1)
             evacuate(nc.scalar.copy, k_sb, 0, r, 1)
             evacuate(nc.scalar.copy, k_sb, 0, r, 2)
             exponent(r)
             for w in range(3):
-                evacuate(nc.vector.tensor_copy, v_sb, 1, r, w)
+                evacuate(nc.scalar.copy, v_sb, 1, r, w)
             passes(r + 1, 0)
             transpose("k", 5, k_sb, r)
-            transpose("v", 7, v_sb, r)
             passes(r + 1, 1)
+            transpose("v", 7, v_sb, r)
             inverse_sum(r)
             context(r)
             relu(r)
@@ -316,15 +312,15 @@ def tile_broadcastattention_w_kernel(tc, x, wq_words, wq_scales, bqkv, wp_words,
         for m in range(4):
             stage2(first[m], m, range(3, 4))
             (out_vector if m % 2 else out_scalar)(m, first[m])
-        store(0)
-        store(2)
+        store(0, 4)
         for j in range(2, 6):
             po = bank(2 + j)
             for i in range(2):
                 stage2(po[:, N * i : N * (i + 1)], 2 * j + i, range(G))
             for i in range(2):
                 (out_vector if j % 2 else out_scalar)(2 * j + i, po[:, N * i : N * (i + 1)])
-            store(2 * j)
+            if j % 2:
+                store(2 * j - 2, 2 * j + 2)
         last = [bank(b)[:, 0:N] for b in range(4)]
         for i in range(4):
             stage2(last[i], 12 + i, range(3))
@@ -332,5 +328,5 @@ def tile_broadcastattention_w_kernel(tc, x, wq_words, wq_scales, bqkv, wp_words,
             stage2(last[i], 12 + i, range(3, 4))
         for i in range(4):
             (out_vector if i % 2 else out_scalar)(12 + i, last[i])
-        store(12)
-        store(14)
+        store(12, 14)
+        store(14, 16)

@@ -74,6 +74,11 @@ def tile_broadcastattention_w_kernel(tc, x, wq_words, wq_scales, bqkv, wp_words,
                 out=pl[32 * q : 32 * q + 16, :].bitcast(I32),
                 in_=wq_scales[:, 4 * q : 4 * q + 4, :].bitcast(I32),
             )
+        for q in range(4):
+            nc.sync.dma_start(
+                out=wp_pl[32 * q : 32 * q + 16, :].bitcast(I32),
+                in_=wp_scales[:, 4 * q : 4 * q + 4, :].bitcast(I32),
+            )
         wq_src = wq_words.rearrange("g p n t -> p g (n t)")
         for r in range(G):
             for kg in range(G):
@@ -81,11 +86,6 @@ def tile_broadcastattention_w_kernel(tc, x, wq_words, wq_scales, bqkv, wp_words,
                     out=wq[:, kg, RC * r : RC * (r + 1)].bitcast(I32),
                     in_=wq_src[:, kg, 4 * RC * r : 4 * RC * (r + 1)].bitcast(I32),
                 )
-        for q in range(4):
-            nc.sync.dma_start(
-                out=wp_pl[32 * q : 32 * q + 16, :].bitcast(I32),
-                in_=wp_scales[:, 4 * q : 4 * q + 4, :].bitcast(I32),
-            )
         wp_src = wp_words.rearrange("g p n t -> p g (n t)")
         for c0, c1, g0, g1 in WP_CHUNKS:
             nc.sync.dma_start(out=wp[:, g0:g1, c0:c1].bitcast(I32), in_=wp_src[:, g0:g1, 4 * c0 : 4 * c1].bitcast(I32))

@@ -24,7 +24,7 @@ G = DIM // 512
 HR = H // G
 RC = HR * R
 WINDOWS = ((0, 512, 0, 15), (480, 512, 15, 30), (928, 128, 30, 32))
-WP_CHUNKS = ((0, 1024, 0, 4), (1024, 1536, 0, 4), (1536, 2048, 0, 3), (1536, 2048, 3, 4))
+WP_CHUNKS = ((0, 1024, 0, 4), (1024, 1536, 0, 4), (1536, 2048, 0, 3), (1536, 1792, 3, 4), (1792, 2048, 3, 4))
 
 FLOPS = 2 * O * DIM * N + 2 * DIM * DIM * N
 
@@ -326,7 +326,6 @@ def tile_broadcastattention_w_kernel(tc, x, wq_words, wq_scales, bqkv, wp_words,
             stage2(last[i], 12 + i, range(3))
         for i in range(4):
             stage2(last[i], 12 + i, range(3, 4))
-        for i in range(4):
             (out_vector if i % 2 else out_scalar)(12 + i, last[i])
-        store(12, 14)
-        store(14, 16)
+            if i % 2:
+                store(11 + i, 13 + i)

@@ -24,7 +24,7 @@ G = DIM // 512
 HR = H // G
 RC = HR * R
 WINDOWS = ((0, 512, 0, 15), (480, 512, 15, 30), (928, 128, 30, 32))
-WP_CHUNKS = ((0, 1024, 0, 4), (1024, 1536, 0, 4), (1536, 2048, 0, 3), (1536, 1792, 3, 4), (1792, 2048, 3, 4))
+WP_CHUNKS = ((0, 1024, 0, 2), (0, 1024, 2, 4), (1024, 1536, 0, 4), (1536, 2048, 0, 3), (1536, 1792, 3, 4), (1792, 2048, 3, 4))
 
 FLOPS = 2 * O * DIM * N + 2 * DIM * DIM * N
 
@@ -165,18 +165,18 @@ def tile_broadcastattention_w_kernel(tc, x, wq_words, wq_scales, bqkv, wp_words,
                 in_=src.unsqueeze(2).to_broadcast([P, HR, 4]),
             )
 
-        def q_passes(r):
-            tl[("tq", r)] = bank(6)[:, 0:P]
-            for kg in range(G):
-                nc.tensor.matmul_mx(
-                    out=tl[("tq", r)],
-                    lhsT=q_w[:, r, kg, :].bitcast(FP8X4),
-                    lhsT_scale=q_pl[4 * kg : P, P * r : P * (r + 1)],
-                    rhs=xw[:, N * kg : N * (kg + 1)].bitcast(FP8X4),
-                    rhs_scale=xs[:, N * kg : N * (kg + 1)],
-                    start=(kg == 0),
-                    stop=(kg == G - 1),
-                )
+        def q_pass(r, kg):
+            if kg == 0:
+                tl[("tq", r)] = bank(6)[:, 0:P]
+            nc.tensor.matmul_mx(
+                out=tl[("tq", r)],
+                lhsT=q_w[:, r, kg, :].bitcast(FP8X4),
+                lhsT_scale=q_pl[4 * kg : P, P * r : P * (r + 1)],
+                rhs=xw[:, N * kg : N * (kg + 1)].bitcast(FP8X4),
+                rhs_scale=xs[:, N * kg : N * (kg + 1)],
+                start=(kg == 0),
+                stop=(kg == G - 1),
+            )
 
         def passes(r, kg):
             if r < G:
@@ -184,11 +184,15 @@ def tile_broadcastattention_w_kernel(tc, x, wq_words, wq_scales, bqkv, wp_words,
                     q_words(r, kg)
                 one_pass(r, 0, kg)
                 if kg == G - 1:
-                    q_passes(r)
+                    q_pass(r, kg)
                 one_pass(r, 1, kg)
-                if kg == G - 1:
-                    for each in range(G):
+                if kg == G - 2:
+                    for each in range(G - 1):
+                        q_pass(r, each)
+                    for each in range(G - 1):
                         one_pass(r, 2, each)
+                if kg == G - 1:
+                    one_pass(r, 2, kg)
 
         def evacuate(copy, dst, part, r, w):
             c, width, h0, h1 = WINDOWS[w]
@@ -304,24 +308,25 @@ def tile_broadcastattention_w_kernel(tc, x, wq_words, wq_scales, bqkv, wp_words,
                 nc.tensor.matmul(out=bp_ps[:, 0:16], lhsT=bpt[:], rhs=ident_b[:, 0:16], start=True, stop=True)
                 nc.scalar.copy(out=bias_p[:], in_=bp_ps[:, 0:16])
             passes(r + 1, 2)
-        first = [bank(b)[:, 0:N] for b in range(4)]
-        for m in range(4):
-            stage2(first[m], m, range(3))
+        early = [bank(b)[:, 0:N] for b in (0, 1, 2, 3, 4, 6, 7, 5)]
+        for groups in (range(2), range(2, 3)):
+            for m in range(8):
+                stage2(early[m], m, groups)
         hidden(G - 1)
         quantise_h(G - 1)
-        for m in range(4):
-            stage2(first[m], m, range(3, 4))
-            (out_vector if m % 2 else out_scalar)(m, first[m])
-        store(0, 4)
-        for j in range(2, 6):
-            po = bank(2 + j)
+        for m in range(8):
+            stage2(early[m], m, range(3, 4))
+            (out_vector if m % 2 else out_scalar)(m, early[m])
+            if m % 4 == 3:
+                store(m - 3, m + 1)
+        for j in (4, 5):
+            po = bank(j - 4)
             for i in range(2):
                 stage2(po[:, N * i : N * (i + 1)], 2 * j + i, range(G))
             for i in range(2):
                 (out_vector if j % 2 else out_scalar)(2 * j + i, po[:, N * i : N * (i + 1)])
-            if j % 2:
-                store(2 * j - 2, 2 * j + 2)
-        last = [bank(b)[:, 0:N] for b in range(4)]
+        store(8, 12)
+        last = [bank(b)[:, 0:N] for b in (2, 3, 4, 6)]
         for i in range(4):
             stage2(last[i], 12 + i, range(3))
         for i in range(4):

@@ -183,8 +183,6 @@ def tile_broadcastattention_w_kernel(tc, x, wq_words, wq_scales, bqkv, wp_words,
                 if kg < G - 1:
                     q_words(r, kg)
                 one_pass(r, 0, kg)
-                if kg == G - 1:
-                    q_pass(r, kg)
                 one_pass(r, 1, kg)
                 if kg == G - 2:
                     for each in range(G - 1):
@@ -192,6 +190,7 @@ def tile_broadcastattention_w_kernel(tc, x, wq_words, wq_scales, bqkv, wp_words,
                     for each in range(G - 1):
                         one_pass(r, 2, each)
                 if kg == G - 1:
+                    q_pass(r, kg)
                     one_pass(r, 2, kg)
 
         def evacuate(copy, dst, part, r, w):
@@ -214,9 +213,11 @@ def tile_broadcastattention_w_kernel(tc, x, wq_words, wq_scales, bqkv, wp_words,
                 out=tl[("e", r)][:], in_=tl[("tq", r)], func=ACT.Exp, bias=tl[("negmax", r)][:, 0:1], scale=1.0, accum_out=tl[("esum", r)][:]
             )
 
-        def inverse_sum(r):
-            tl[("rsum", r)] = work.tile([P, 1], F32, tag="rsum", name="rsum")
-            nc.vector.reciprocal(out=tl[("rsum", r)][:], in_=tl[("esum", r)][:])
+        def normalise(r):
+            rsum = work.tile([P, 1], F32, tag="rsum")
+            nc.vector.reciprocal(out=rsum[:], in_=tl[("esum", r)][:])
+            tl[("s", r)] = work.tile([P, N], F32, tag="s", name="scores")
+            nc.vector.tensor_scalar_mul(out=tl[("s", r)][:], in0=tl[("e", r)][:], scalar1=rsum[:, 0:1])
 
         def transpose(key, b, src, r):
             tl[(key, r)] = bank(b)[:].rearrange("p (t n) -> p t n", t=4)
@@ -224,16 +225,18 @@ def tile_broadcastattention_w_kernel(tc, x, wq_words, wq_scales, bqkv, wp_words,
                 nc.tensor.transpose(out=tl[(key, r)][:, t, :], in_=src[:, t, P * r : P * (r + 1)], identity=ident_f[:])
 
         def context(r):
-            acc = work.tile([P, 4], F32, tag="acc")
+            tl[("ctx", r)] = work.tile([P, 4], F32, tag="ctx", name="ctx_sb")
             product = work.tile([P, N], F32, tag="product")
             for t in range(4):
                 nc.vector.scalar_tensor_tensor(
-                    out=product[:], in0=tl[("k", r)][:, t, :], scalar=1.0, in1=tl[("e", r)][:], op0=ALU.mult, op1=ALU.mult, accum_out=acc[:, t : t + 1]
+                    out=product[:],
+                    in0=tl[("k", r)][:, t, :],
+                    scalar=bias_kv[:, 2 * r, t : t + 1],
+                    in1=tl[("s", r)][:],
+                    op0=ALU.add,
+                    op1=ALU.mult,
+                    accum_out=tl[("ctx", r)][:, t : t + 1],
                 )
-            tl[("ctx", r)] = work.tile([P, 4], F32, tag="ctx", name="ctx_sb")
-            nc.vector.scalar_tensor_tensor(
-                out=tl[("ctx", r)][:], in0=acc[:], scalar=tl[("rsum", r)][:, 0:1], in1=bias_kv[:, 2 * r, :], op0=ALU.mult, op1=ALU.add
-            )
 
         def relu(r):
             tl[("relu", r)] = work.tile([P, 4, N], F32, tag="relu", name="relu_v")
@@ -286,27 +289,28 @@ def tile_broadcastattention_w_kernel(tc, x, wq_words, wq_scales, bqkv, wp_words,
         for r in range(G):
             q_words(r, G - 1)
             passes(r, G - 1)
-            evacuate(nc.vector.tensor_copy, k_sb, 0, r, 0)
-            row_max(r)
+            if r == 0:
+                bp_ps = bank(5)
+                nc.tensor.matmul(out=bp_ps[:, 0:16], lhsT=bpt[:], rhs=ident_b[:, 0:16], start=True, stop=True)
+                nc.scalar.copy(out=bias_p[:], in_=bp_ps[:, 0:16])
             if r > 0:
                 hidden(r - 1)
+            row_max(r)
+            if r > 0:
                 quantise_h(r - 1)
-            evacuate(nc.scalar.copy, k_sb, 0, r, 1)
-            evacuate(nc.scalar.copy, k_sb, 0, r, 2)
-            exponent(r)
             for w in range(3):
+                evacuate(nc.scalar.copy, k_sb, 0, r, w)
+            exponent(r)
+            evacuate(nc.vector.tensor_copy, v_sb, 1, r, 0)
+            for w in (1, 2):
                 evacuate(nc.scalar.copy, v_sb, 1, r, w)
             passes(r + 1, 0)
             transpose("k", 5, k_sb, r)
             passes(r + 1, 1)
             transpose("v", 7, v_sb, r)
-            inverse_sum(r)
+            normalise(r)
             context(r)
             relu(r)
-            if r == 1:
-                bp_ps = bank(5)
-                nc.tensor.matmul(out=bp_ps[:, 0:16], lhsT=bpt[:], rhs=ident_b[:, 0:16], start=True, stop=True)
-                nc.scalar.copy(out=bias_p[:], in_=bp_ps[:, 0:16])
             passes(r + 1, 2)
         early = [bank(b)[:, 0:N] for b in (0, 1, 2, 3, 4, 6, 7, 5)]
         for groups in (range(2), range(2, 3)):

@@ -24,7 +24,7 @@ G = DIM // 512
 HR = H // G
 RC = HR * R
 WINDOWS = ((0, 512, 0, 15), (480, 512, 15, 30), (928, 128, 30, 32))
-WP_CHUNKS = ((0, 1024, 0, 2), (0, 1024, 2, 4), (1024, 1536, 0, 4), (1536, 2048, 0, 3), (1536, 1792, 3, 4), (1792, 2048, 3, 4))
+WP_CHUNKS = ((0, 1024, 0, 2), (0, 1024, 2, 4), (1024, 2048, 0, 2), (1024, 2048, 2, 3), (1024, 1536, 3, 4), (1536, 1792, 3, 4), (1792, 2048, 3, 4))
 
 FLOPS = 2 * O * DIM * N + 2 * DIM * DIM * N
 
@@ -323,18 +323,12 @@ def tile_broadcastattention_w_kernel(tc, x, wq_words, wq_scales, bqkv, wp_words,
             (out_vector if m % 2 else out_scalar)(m, early[m])
             if m % 4 == 3:
                 store(m - 3, m + 1)
-        for j in (4, 5):
-            po = bank(j - 4)
-            for i in range(2):
-                stage2(po[:, N * i : N * (i + 1)], 2 * j + i, range(G))
-            for i in range(2):
-                (out_vector if j % 2 else out_scalar)(2 * j + i, po[:, N * i : N * (i + 1)])
-        store(8, 12)
-        last = [bank(b)[:, 0:N] for b in (2, 3, 4, 6)]
-        for i in range(4):
-            stage2(last[i], 12 + i, range(3))
-        for i in range(4):
-            stage2(last[i], 12 + i, range(3, 4))
-            (out_vector if i % 2 else out_scalar)(12 + i, last[i])
-            if i % 2:
-                store(11 + i, 13 + i)
+        late = [bank(b)[:, 0:N] for b in (0, 1, 2, 3, 4, 6, 7, 5)]
+        for groups in (range(2), range(2, 3)):
+            for i in range(8):
+                stage2(late[i], 8 + i, groups)
+        for m0, m1 in ((8, 12), (12, 14), (14, 16)):
+            for m in range(m0, m1):
+                stage2(late[m - 8], m, range(3, 4))
+                (out_vector if m % 2 else out_scalar)(m, late[m - 8])
+            store(m0, m1)

from contextlib import ExitStack

import concourse.mybir as mybir
from concourse.masks import make_identity

F32 = mybir.dt.float32
BF16 = mybir.dt.bfloat16
I32 = mybir.dt.int32
U32 = mybir.dt.uint32
U8 = mybir.dt.uint8
FP8X4 = mybir.dt.float8_e4m3fn_x4
ALU = mybir.AluOpType
ACT = mybir.ActivationFunctionType
AX = mybir.AxisListType

P = 128
N = 128
DIM = 2048
H = 128
HD = 16
R = 1 + 2 * HD
O = H * R
G = DIM // 512
HR = H // G
RC = HR * R
WINDOWS = ((0, 512, 0, 15), (480, 512, 15, 30), (928, 128, 30, 32))
WP_CHUNKS = ((0, 1024, 0, 2), (0, 1024, 2, 4), (1024, 2048, 0, 2), (1024, 2048, 2, 3), (1024, 1536, 3, 4), (1536, 1792, 3, 4), (1792, 2048, 3, 4))

FLOPS = 2 * O * DIM * N + 2 * DIM * DIM * N


def tile_broadcastattention_w_kernel(tc, x, wq_words, wq_scales, bqkv, wp_words, wp_scales, bp, out):
    nc = tc.nc
    with ExitStack() as ctx:
        ctx.enter_context(tc.manual_schedule())
        keep = ctx.enter_context(tc.tile_pool(name="keep", bufs=1))
        work = ctx.enter_context(tc.tile_pool(name="work", bufs=2))
        psum = ctx.enter_context(tc.psum_pool(name="psum", bufs=1))

        def bank(i):
            return psum.tile([P, 512], F32, tag="b%d" % i, name="bank")

        pl = keep.tile([P, O], U8, align_bytes=64)
        pl2 = keep.tile([P, O + 64], U8, align_bytes=64)
        q_pl = keep.tile([P, 4 * H], U8, align_bytes=64)
        wp_pl = keep.tile([P, DIM], U8, align_bytes=64)
        wq = keep.tile([P, G, O], U32, align_bytes=64)
        q_w = keep.tile([P, G, G, 4 * HR], U32, align_bytes=64)
        wp = keep.tile([P, G, DIM], U32, align_bytes=64)
        xraw = keep.tile([P, G, 4 * N], BF16)
        bq = keep.tile([P, R], BF16)
        bpt = keep.tile([P, P], BF16)
        warm_in = keep.tile([P, 1], F32)
        dummy = keep.tile([P, 512], BF16)
        warm_out = keep.tile([P, 1], F32)
        ident_f = keep.tile([P, P], F32)
        ident_b = keep.tile([P, P], BF16)

        nc.vector.memset(warm_in[:], 0.0)
        nc.vector.memset(pl[:].bitcast(I32), 0)
        nc.vector.memset(dummy[:].bitcast(F32), 0.0)
        nc.vector.memset(wp_pl[:].bitcast(I32), 0)
        nc.scalar.activation(out=warm_out[:], in_=warm_in[:], func=ACT.Exp)

        nc.gpsimd.dma_start(out=bq[:], in_=bqkv.rearrange("(h r) -> h r", r=R))
        nc.gpsimd.memset(bpt[:], 0.0)
        nc.gpsimd.dma_start(out=bpt[0:16, :], in_=bp.rearrange("(m p) -> m p", p=P))
        make_identity(nc, ident_b[:])
        make_identity(nc, ident_f[:])

        nc.sync.dma_start(out=xraw[:], in_=x[0].rearrange("(g p j) n -> p g (j n)", g=G, p=P, j=4))
        for q in range(4):
            nc.sync.dma_start(
                out=pl[32 * q : 32 * q + 16, :].bitcast(I32),
                in_=wq_scales[:, 4 * q : 4 * q + 4, :].bitcast(I32),
            )
        for q in range(4):
            nc.sync.dma_start(
                out=wp_pl[32 * q : 32 * q + 16, :].bitcast(I32),
                in_=wp_scales[:, 4 * q : 4 * q + 4, :].bitcast(I32),
            )
        wq_src = wq_words.rearrange("g p n t -> p g (n t)")
        for r in range(G):
            for kg in range(G):
                nc.sync.dma_start(
                    out=wq[:, kg, RC * r : RC * (r + 1)].bitcast(I32),
                    in_=wq_src[:, kg, 4 * RC * r : 4 * RC * (r + 1)].bitcast(I32),
                )
        wp_src = wp_words.rearrange("g p n t -> p g (n t)")
        for c0, c1, g0, g1 in WP_CHUNKS:
            nc.sync.dma_start(out=wp[:, g0:g1, c0:c1].bitcast(I32), in_=wp_src[:, g0:g1, 4 * c0 : 4 * c1].bitcast(I32))

        xg = keep.tile([P, G, N, 4], BF16, align_bytes=64)
        for half in range(2):
            nc.vector.tensor_copy(
                out=xg[:, 2 * half : 2 * half + 2, :, :],
                in_=xraw[:, 2 * half : 2 * half + 2, :].rearrange("p g (j n) -> p g n j", j=4),
            )
        xw = keep.tile([P, G * N], U32, align_bytes=64)
        xs = keep.tile([P, G * N], U8, align_bytes=64)
        for half in range(2):
            nc.vector.quantize_mx(
                out=xw[:, 2 * N * half : 2 * N * (half + 1)].bitcast(FP8X4),
                scales=xs[:, 2 * N * half : 2 * N * (half + 1)],
                in_=xg[:, 2 * half : 2 * half + 2, :, :].rearrange("p g n j -> p (g n j)"),
            )

        sel = keep.tile([P, 4 * H], BF16)
        nc.vector.tensor_copy(out=sel[:].rearrange("p (h a) -> p h a", a=4), in_=ident_b[:].unsqueeze(2).to_broadcast([P, H, 4]))
        mask = keep.tile([P, 4], F32)
        nc.vector.tensor_reduce(out=mask[:], in_=ident_f[:].rearrange("p (h a) -> p a h", a=4), axis=AX.X, op=ALU.add)
        bias_ps = bank(5)

        def warm_up(count):
            for i in range(count):
                nc.tensor.matmul(out=bank(i % 4)[:], lhsT=dummy[:, 0:P], rhs=dummy[:], start=True, stop=True)

        warm_up(8)
        for r in range(G):
            nc.tensor.matmul(out=bias_ps[:, 32 * r : 32 * (r + 1)], lhsT=sel[:, P * r : P * (r + 1)], rhs=bq[:, 1:R], start=True, stop=True)
        warm_up(4)
        nc.vector.tensor_copy(out=pl2[:].bitcast(I32)[:, 8 : 8 + O // 4], in_=pl[:].bitcast(I32))
        for a in range(4):
            nc.vector.tensor_copy(out=q_pl[:, a : 4 * H : 4], in_=pl[:, 0 : O : R])

        masked = keep.tile([P, 8, 4, 4], F32)
        bias_kv = keep.tile([P, 8, 4], F32)
        bias_p = keep.tile([P, 16], F32)
        nc.vector.tensor_tensor(
            out=masked[:],
            in0=bias_ps[:, 0:P].rearrange("p (q a t) -> p q a t", a=4, t=4),
            in1=mask[:].unsqueeze(1).unsqueeze(3).to_broadcast([P, 8, 4, 4]),
            op=ALU.mult,
        )
        nc.vector.tensor_reduce(out=bias_kv[:], in_=masked[:].rearrange("p q a t -> p q t a"), axis=AX.X, op=ALU.add)

        k_sb = keep.tile([P, 4, 4 * H], F32)
        v_sb = keep.tile([P, 4, 4 * H], F32)
        hg = keep.tile([P, G, N, 4], BF16, align_bytes=64)
        hw = keep.tile([P, G * N], U32, align_bytes=64)
        hs = keep.tile([P, G * N], U8, align_bytes=64)
        win = {}
        tl = {}

        def one_pass(r, w, kg):
            c, width, h0, h1 = WINDOWS[w]
            if kg == 0:
                win[(r, w)] = bank(2 * (r % 2) + w if w < 2 else 4)
            col = RC * r + c
            plane, pc = (pl, col) if col % 64 == 0 else (pl2, col + 32)
            nc.tensor.matmul_mx(
                out=win[(r, w)][:, 0:width],
                lhsT=xw[:, N * kg : N * (kg + 1)].bitcast(FP8X4),
                lhsT_scale=xs[:, N * kg : N * (kg + 1)],
                rhs=wq[:, kg, col : col + width].bitcast(FP8X4),
                rhs_scale=plane[4 * kg : P, pc : pc + width],
                start=(kg == 0),
                stop=(kg == G - 1),
            )

        def q_words(r, kg):
            src = wq[:, kg, RC * r : RC * (r + 1) : R].bitcast(I32)
            (nc.vector if kg == r == G - 1 else nc.gpsimd).tensor_copy(
                out=q_w[:, r, kg, :].bitcast(I32).rearrange("p (h a) -> p h a", a=4),
                in_=src.unsqueeze(2).to_broadcast([P, HR, 4]),
            )

        def q_pass(r, kg):
            if kg == 0:
                tl[("tq", r)] = bank(6)[:, 0:P]
            nc.tensor.matmul_mx(
                out=tl[("tq", r)],
                lhsT=q_w[:, r, kg, :].bitcast(FP8X4),
                lhsT_scale=q_pl[4 * kg : P, P * r : P * (r + 1)],
                rhs=xw[:, N * kg : N * (kg + 1)].bitcast(FP8X4),
                rhs_scale=xs[:, N * kg : N * (kg + 1)],
                start=(kg == 0),
                stop=(kg == G - 1),
            )

        def passes(r, kg):
            if r < G:
                if kg < G - 1:
                    q_words(r, kg)
                one_pass(r, 0, kg)
                one_pass(r, 1, kg)
                if kg == G - 2:
                    for each in range(G - 1):
                        q_pass(r, each)
                    for each in range(G - 1):
                        one_pass(r, 2, each)
                if kg == G - 1:
                    q_pass(r, kg)
                    one_pass(r, 2, kg)

        def evacuate(copy, dst, part, r, w):
            c, width, h0, h1 = WINDOWS[w]
            off = R * h0 - c
            heads = win[(r, w)][:, off : off + R * (h1 - h0)].rearrange("p (h r) -> p h r", r=R)
            copy(
                out=dst[:, :, 4 * (HR * r + h0) : 4 * (HR * r + h1)].rearrange("p t (h a) -> p t h a", a=4),
                in_=heads[:, :, 1 + HD * part : 1 + HD * (part + 1)].rearrange("p h (a t) -> p t h a", t=4),
            )

        def row_max(r):
            tl[("negmax", r)] = work.tile([P, 1], F32, tag="negmax", name="negmax")
            nc.vector.tensor_reduce(out=tl[("negmax", r)][:], in_=tl[("tq", r)], axis=AX.X, op=ALU.max, negate=True)

        def exponent(r):
            tl[("e", r)] = work.tile([P, N], F32, tag="e", name="e_sb")
            tl[("esum", r)] = work.tile([P, 1], F32, tag="esum", name="esum")
            nc.scalar.activation(
                out=tl[("e", r)][:], in_=tl[("tq", r)], func=ACT.Exp, bias=tl[("negmax", r)][:, 0:1], scale=1.0, accum_out=tl[("esum", r)][:]
            )

        def normalise(r):
            rsum = work.tile([P, 1], F32, tag="rsum")
            nc.vector.reciprocal(out=rsum[:], in_=tl[("esum", r)][:])
            tl[("s", r)] = work.tile([P, N], F32, tag="s", name="scores")
            nc.vector.tensor_scalar_mul(out=tl[("s", r)][:], in0=tl[("e", r)][:], scalar1=rsum[:, 0:1])

        def transpose(key, b, src, r):
            tl[(key, r)] = bank(b)[:].rearrange("p (t n) -> p t n", t=4)
            for t in range(4):
                nc.tensor.transpose(out=tl[(key, r)][:, t, :], in_=src[:, t, P * r : P * (r + 1)], identity=ident_f[:])

        def context(r):
            tl[("ctx", r)] = work.tile([P, 4], F32, tag="ctx", name="ctx_sb")
            product = work.tile([P, N], F32, tag="product")
            for t in range(4):
                nc.vector.scalar_tensor_tensor(
                    out=product[:],
                    in0=tl[("k", r)][:, t, :],
                    scalar=bias_kv[:, 2 * r, t : t + 1],
                    in1=tl[("s", r)][:],
                    op0=ALU.add,
                    op1=ALU.mult,
                    accum_out=tl[("ctx", r)][:, t : t + 1],
                )

        def relu(r):
            tl[("relu", r)] = work.tile([P, 4, N], F32, tag="relu", name="relu_v")
            for t in range(4):
                nc.scalar.activation(
                    out=tl[("relu", r)][:, t, :], in_=tl[("v", r)][:, t, :], func=ACT.Relu, bias=bias_kv[:, 2 * r + 1, t : t + 1], scale=1.0
                )

        def hidden(r):
            nc.vector.tensor_tensor(
                out=hg[:, r, :, :],
                in0=tl[("relu", r)][:].rearrange("p t n -> p n t"),
                in1=tl[("ctx", r)][:].unsqueeze(1).to_broadcast([P, N, 4]),
                op=ALU.mult,
            )

        def quantise_h(r):
            nc.vector.quantize_mx(
                out=hw[:, N * r : N * (r + 1)].bitcast(FP8X4),
                scales=hs[:, N * r : N * (r + 1)],
                in_=hg[:, r, :, :].rearrange("p n t -> p (n t)"),
            )

        out_sb = keep.tile([P, 16, N], F32)
        out_v = out[0].rearrange("(m p) n -> p m n", p=P)

        def stage2(dst, m, groups):
            for g in groups:
                nc.tensor.matmul_mx(
                    out=dst,
                    lhsT=wp[:, g, P * m : P * (m + 1)].bitcast(FP8X4),
                    lhsT_scale=wp_pl[4 * g : P, P * m : P * (m + 1)],
                    rhs=hw[:, N * g : N * (g + 1)].bitcast(FP8X4),
                    rhs_scale=hs[:, N * g : N * (g + 1)],
                    start=(g == 0),
                    stop=(g == G - 1),
                )

        def out_scalar(m, src):
            nc.scalar.activation(out=out_sb[:, m, :], in_=src, func=ACT.Identity, bias=bias_p[:, m : m + 1], scale=1.0)

        def out_vector(m, src):
            nc.vector.tensor_scalar_add(out=out_sb[:, m, :], in0=src, scalar1=bias_p[:, m : m + 1])

        def store(m0, m1):
            nc.sync.dma_start(out=out_v[:, m0:m1, :], in_=out_sb[:, m0:m1, :])

        for kg in range(G - 1):
            passes(0, kg)
        for r in range(G):
            q_words(r, G - 1)
            passes(r, G - 1)
            if r == 0:
                bp_ps = bank(5)
                nc.tensor.matmul(out=bp_ps[:, 0:16], lhsT=bpt[:], rhs=ident_b[:, 0:16], start=True, stop=True)
                nc.scalar.copy(out=bias_p[:], in_=bp_ps[:, 0:16])
            if r > 0:
                hidden(r - 1)
            row_max(r)
            if r > 0:
                quantise_h(r - 1)
            for w in range(3):
                evacuate(nc.scalar.copy, k_sb, 0, r, w)
            exponent(r)
            evacuate(nc.vector.tensor_copy, v_sb, 1, r, 0)
            for w in (1, 2):
                evacuate(nc.scalar.copy, v_sb, 1, r, w)
            passes(r + 1, 0)
            transpose("k", 5, k_sb, r)
            passes(r + 1, 1)
            transpose("v", 7, v_sb, r)
            normalise(r)
            context(r)
            relu(r)
            passes(r + 1, 2)
        early = [bank(b)[:, 0:N] for b in (0, 1, 2, 3, 4, 6, 7, 5)]
        for groups in (range(2), range(2, 3)):
            for m in range(8):
                stage2(early[m], m, groups)
        hidden(G - 1)
        quantise_h(G - 1)
        for m in range(8):
            stage2(early[m], m, range(3, 4))
            (out_vector if m % 2 else out_scalar)(m, early[m])
            if m % 4 == 3:
                store(m - 3, m + 1)
        late = [bank(b)[:, 0:N] for b in (0, 1, 2, 3, 4, 6, 7, 5)]
        for groups in (range(2), range(2, 3)):
            for i in range(8):
                stage2(late[i], 8 + i, groups)
        for m0, m1 in ((8, 12), (12, 14), (14, 16)):
            for m in range(m0, m1):
                stage2(late[m - 8], m, range(3, 4))
                (out_vector if m % 2 else out_scalar)(m, late[m - 8])
            store(m0, m1)
